import numpy as np
import ml_dtypes


def mxq(x, axis, fmt="e4m3"):
    dtype, down = {"e4m3": (ml_dtypes.float8_e4m3fn, 7), "e5m2": (ml_dtypes.float8_e5m2, 14)}[fmt]
    v = np.moveaxis(np.asarray(x, np.float32).astype(ml_dtypes.bfloat16).astype(np.float64), axis, -1)
    blocks = v.reshape(v.shape[:-1] + (-1, 32))
    amax = np.abs(blocks).max(-1, keepdims=True)
    byte = np.maximum(np.where(amax > 0, np.frexp(amax)[1] - 1 + 127, 0) - down, 1)
    scale = np.exp2(byte - 127.0)
    codes = (blocks / scale).astype(np.float32).astype(dtype).astype(np.float64)
    return np.moveaxis((codes * scale).reshape(v.shape), -1, axis)


WIDE = False


def mx_kscale(k):
    if not WIDE:
        return np.ones(k)
    levels = np.array([10, -10, 5, -5, 0])
    if k % 512:
        return np.exp2(np.random.permutation(np.resize(levels, k // 32))).repeat(32)
    a = np.empty((k // 512, 16))
    for p in range(k // 512):
        a[p, :8] = np.random.permutation(np.resize(levels, 8))
        for g in range(8):
            far = levels[np.abs(levels - a[p, g]) >= 10]
            a[p, g + 8] = far[np.random.randint(len(far))]
    return np.exp2(a.ravel()).repeat(32)


BF16 = ml_dtypes.bfloat16


def bf(x):
    return np.asarray(x, np.float32).astype(BF16)


def f64(x):
    return np.asarray(x).astype(np.float64)


B, DI, DH, H, DP = 4096, 512, 256, 2, 1536
HD = DH // H
EPS = 1e-5


def sigmoid(v):
    return 1.0 / (1.0 + np.exp(-v))


def setup_inputs():
    s = mx_kscale(DI)
    d = {"x": bf(np.random.standard_normal((B, DI)) * 1.5 + np.random.standard_normal((B, 1)) * 0.5),
         "h_prev": bf(np.random.standard_normal((B, DH)) * 0.5),
         "c_prev": bf(np.random.standard_normal((B, DH))),
         "n_prev": bf(0.5 + np.abs(np.random.standard_normal((B, DH)))),
         "m_prev": bf(np.random.standard_normal((B, DH))),
         "ln_w": bf((1.0 + 0.1 * np.random.standard_normal(DI)) * s),
         "ln_b": bf(0.2 * np.random.standard_normal(DI) * s)}
    for g in "zifo":
        d["W" + g] = bf(np.random.standard_normal((DI, DH)) / np.sqrt(DI) / s[:, None])
        d["b_" + g] = bf(0.2 * np.random.standard_normal(DH))
        d["R" + g] = bf(np.random.standard_normal((H, HD, HD)) / np.sqrt(HD))
        d["rb_" + g] = bf(0.2 * np.random.standard_normal(DH))
    return d


def reference(x, h_prev, c_prev, n_prev, m_prev, ln_w, ln_b,
              Wz, b_z, Rz, rb_z, Wi, b_i, Ri, rb_i, Wf, b_f, Rf, rb_f, Wo, b_o, Ro, rb_o):
    x = f64(x)
    mu = x.mean(-1, keepdims=True)
    var = x.var(-1, keepdims=True)
    xn = (x - mu) / np.sqrt(var + EPS) * f64(ln_w) + f64(ln_b)
    xq = mxq(xn, 1, "e4m3")
    hr = f64(h_prev).reshape(B, H, HD).transpose(1, 0, 2)

    def gate(W, b, R, rb):
        rec = (hr @ f64(R)).transpose(1, 0, 2).reshape(B, DH)
        return (xq @ mxq(f64(W), 0, "e4m3")) + f64(b) + (rec + f64(rb))

    z_t = gate(Wz, b_z, Rz, rb_z)
    i_t = gate(Wi, b_i, Ri, rb_i)
    f_t = gate(Wf, b_f, Rf, rb_f)
    o_t = gate(Wo, b_o, Ro, rb_o)
    zt = np.tanh(z_t)
    ot = sigmoid(o_t)
    mt = np.maximum(f_t + f64(m_prev), i_t)
    it = np.exp(i_t - mt)
    ft = np.exp(f_t + f64(m_prev) - mt)
    ct = ft * f64(c_prev) + it * zt
    nt = ft * f64(n_prev) + it
    ht = ot * (ct / (nt + 1e-13))
    return (ht, ct, nt, mt)

@@ -1,0 +1,323 @@
+from contextlib import ExitStack
+
+import concourse.mybir as mybir
+from concourse.masks import make_identity
+
+F32 = mybir.dt.float32
+BF16 = mybir.dt.bfloat16
+U32 = mybir.dt.uint32
+U8 = mybir.dt.uint8
+FP8X4 = mybir.dt.float8_e4m3fn_x4
+ALU = mybir.AluOpType
+ACT = mybir.ActivationFunctionType
+
+P = 128
+PACK = 4
+ROWS = 4096
+D_IN = 512
+D_HID = 256
+HEADS = 2
+D_HEAD = 128
+GATES = 4
+BLOCKS = GATES * HEADS
+LN_EPS = 1e-5
+DIV_EPS = 1e-13
+
+TILES = 4
+CHUNK = TILES * P
+N_CHUNKS = ROWS // CHUNK
+PAIR = 2
+N_PAIRS = TILES // PAIR
+
+FLOPS = 2 * ROWS * D_IN * GATES * D_HID + 2 * ROWS * D_HEAD * GATES * D_HID
+
+
+def tile_slstmblock_pa_t_kernel(
+    tc, x, h_prev, c_prev, n_prev, m_prev, ln_w, ln_b,
+    Wz, b_z, Rz, rb_z, Wi, b_i, Ri, rb_i, Wf, b_f, Rf, rb_f, Wo, b_o, Ro, rb_o,
+    out_0, out_1, out_2, out_3,
+):
+    nc = tc.nc
+    weights = [Wz, Wi, Wf, Wo]
+    recurrents = [Rz, Ri, Rf, Ro]
+    biases = [b_z, b_i, b_f, b_o]
+    rec_biases = [rb_z, rb_i, rb_f, rb_o]
+    GZ, GI, GF, GO = 0, 1, 2, 3
+
+    def chunk_rows(dram, s):
+        return dram[s * CHUNK:(s + 1) * CHUNK, :].rearrange("(p j) w -> p j w", j=TILES)
+
+    with ExitStack() as stack:
+        const = stack.enter_context(tc.tile_pool(name="const", bufs=1))
+        keep = stack.enter_context(tc.tile_pool(name="keep", bufs=1))
+        loads = stack.enter_context(tc.tile_pool(name="loads", bufs=2))
+        psum_pre = stack.enter_context(tc.psum_pool(name="psum_pre", bufs=1))
+        psum_rot = stack.enter_context(tc.psum_pool(name="psum_rot", bufs=2))
+
+        ident_f32 = const.tile([P, P], F32)
+        make_identity(nc, ident_f32[:])
+        ident_bf16 = const.tile([P, P], BF16)
+        make_identity(nc, ident_bf16[:])
+        neg_half = const.tile([P, TILES], F32)
+        nc.vector.memset(neg_half[:], -0.5)
+        div_eps = const.tile([P, 1], F32)
+        nc.vector.memset(div_eps[:], DIV_EPS)
+
+        vec_rows = const.tile([P, P], BF16)
+        nc.vector.memset(vec_rows[:], 0.0)
+        ln_rows = const.tile([P, 1, PACK], BF16)
+        nc.scalar.dma_start(out=ln_rows[:, 0, :], in_=ln_w.rearrange("(p t) -> p t", t=PACK))
+        ln_rows_b = const.tile([P, 1, PACK], BF16)
+        nc.scalar.dma_start(out=ln_rows_b[:, 0, :], in_=ln_b.rearrange("(p t) -> p t", t=PACK))
+        for g in range(GATES):
+            nc.scalar.dma_start(out=vec_rows[8 + HEADS * g:8 + HEADS * (g + 1), :],
+                                in_=biases[g].rearrange("(h f) -> h f", f=D_HEAD))
+            nc.scalar.dma_start(out=vec_rows[16 + HEADS * g:16 + HEADS * (g + 1), :],
+                                in_=rec_biases[g].rearrange("(h f) -> h f", f=D_HEAD))
+
+        x_tiles = {}
+        h_tiles = {}
+        c_tiles = {}
+        n_tiles = {}
+        m_tiles = {}
+
+        def load_x(s):
+            x_sb = loads.tile([P, TILES, D_IN], BF16, tag="x_sb", bufs=3)
+            nc.sync.dma_start(out=x_sb[:], in_=chunk_rows(x, s))
+            x_tiles[s] = x_sb
+
+        def load_state(s):
+            h_sb = loads.tile([P, TILES, D_HID], BF16, tag="h_sb")
+            nc.sync.dma_start(out=h_sb[:], in_=chunk_rows(h_prev, s))
+            h_tiles[s] = h_sb
+            m_sb = loads.tile([P, TILES, D_HID], BF16, tag="m_sb")
+            nc.sync.dma_start(out=m_sb[:], in_=chunk_rows(m_prev, s))
+            m_tiles[s] = m_sb
+            c_sb = loads.tile([P, TILES, D_HID], BF16, tag="c_sb")
+            nc.sync.dma_start(out=c_sb[:], in_=chunk_rows(c_prev, s))
+            c_tiles[s] = c_sb
+            n_sb = loads.tile([P, TILES, D_HID], BF16, tag="n_sb")
+            nc.sync.dma_start(out=n_sb[:], in_=chunk_rows(n_prev, s))
+            n_tiles[s] = n_sb
+
+        load_x(0)
+
+        w_codes = const.tile([P, GATES * D_HID], U32, align_bytes=64)
+        w_scales = const.tile([P, GATES * D_HID], U8, align_bytes=64)
+        r_sb = const.tile([P, GATES, HEADS, D_HEAD], BF16)
+        with tc.tile_pool(name="setup", bufs=2) as setup:
+            for g in range(GATES):
+                w_raw = setup.tile([P, PACK, D_HID], BF16)
+                nc.sync.dma_start(out=w_raw[:], in_=weights[g].rearrange("(p t) f -> p t f", t=PACK))
+                w_grouped = setup.tile([P, D_HID, PACK], BF16, align_bytes=64)
+                nc.scalar.copy(out=w_grouped[:], in_=w_raw[:].rearrange("p t f -> p f t"))
+                cols = slice(g * D_HID, (g + 1) * D_HID)
+                nc.vector.quantize_mx(
+                    out=w_codes[:, cols].bitcast(FP8X4),
+                    scales=w_scales[:, cols],
+                    in_=w_grouped[:].rearrange("p f t -> p (f t)"),
+                )
+        load_x(1)
+        load_state(0)
+        for g in range(GATES):
+            nc.sync.dma_start(out=r_sb[:, g, :, :], in_=recurrents[g].rearrange("h k f -> k h f"))
+        load_x(2)
+
+        vec_ps = psum_rot.tile([P, P], BF16, tag="turn")
+        nc.tensor.transpose(vec_ps[:], vec_rows[:], ident_bf16[:])
+        vec_cols = const.tile([P, 24], F32)
+        nc.vector.tensor_copy(out=vec_cols[:], in_=vec_ps[:, 0:24])
+        ln_cols = const.tile([P, 2 * PACK], F32)
+        nc.vector.tensor_copy(out=ln_cols[:, 0:PACK], in_=ln_rows[:, 0, :])
+        nc.vector.tensor_copy(out=ln_cols[:, PACK:2 * PACK], in_=ln_rows_b[:, 0, :])
+        gain = ln_cols[:, 0:PACK]
+        shift = ln_cols[:, PACK:2 * PACK]
+        gate_bias = const.tile([P, BLOCKS], F32)
+        nc.vector.tensor_add(out=gate_bias[:], in0=vec_cols[:, 8:16], in1=vec_cols[:, 16:24])
+
+        nt_keep = [keep.tile([P, TILES, D_HID], F32, name="nt_keep%d" % s) for s in range(N_CHUNKS)]
+        oc_keep = [keep.tile([P, TILES, D_HID], F32, name="oc_keep%d" % s) for s in range(N_CHUNKS)]
+        sg_keep = [keep.tile([P, TILES, D_HID], BF16, name="sg_keep%d" % s) for s in range(N_CHUNKS)]
+
+        with ExitStack() as main_stack:
+            products = main_stack.enter_context(
+                tc.tile_pool(name="products", bufs=2, reuse_waits="tile"))
+            work = main_stack.enter_context(tc.tile_pool(name="work", bufs=2, reuse_waits="tile"))
+            xh_tiles = {}
+            x_mx = {}
+            ht_tiles = {}
+            mt_tiles = {}
+            m_out = {}
+            c_out = {}
+
+            def normalise(s):
+                x_sb = x_tiles.pop(s)
+                stats = work.tile([P, TILES, 6], F32, tag="stats")
+                mean_var = work.tile([P, TILES, 2], F32, tag="mean_var")
+                for j in range(TILES):
+                    nc.vector.bn_stats(out=stats[:, j, :], in_=x_sb[:, j, :])
+                for j in range(TILES):
+                    nc.vector.bn_aggr(out=mean_var[:, j, :], in_=stats[:, j, :])
+                var_eps = work.tile([P, TILES], F32, tag="var_eps")
+                nc.vector.tensor_scalar_add(out=var_eps[:], in0=mean_var[:, :, 1], scalar1=LN_EPS)
+                neg_mean = work.tile([P, TILES], F32, tag="neg_mean")
+                nc.vector.tensor_scalar_mul(out=neg_mean[:], in0=mean_var[:, :, 0], scalar1=-1.0)
+                rstd = work.tile([P, TILES], F32, tag="rstd")
+                nc.gpsimd.tensor_tensor(out=rstd[:], in0=var_eps[:], in1=neg_half[:], op=ALU.pow)
+                xh = []
+                for j in range(TILES):
+                    xh_j = work.tile([P, D_IN], F32, tag="xh", bufs=2 * TILES)
+                    nc.gpsimd.tensor_scalar(out=xh_j[:].rearrange("p (t k) -> p t k", t=PACK),
+                                            in0=x_sb[:, j, :].rearrange("p (k t) -> p t k", t=PACK),
+                                            scalar1=neg_mean[:, j:j + 1], scalar2=rstd[:, j:j + 1],
+                                            op0=ALU.add, op1=ALU.mult)
+                    xh.append(xh_j)
+                xh_tiles[s] = xh
+
+            def quantise_xn(s):
+                xh = xh_tiles.pop(s)
+                xn_planes = work.tile([P, PACK, CHUNK], BF16, tag="xn_planes", bufs=1)
+                for t in range(PACK):
+                    turned = psum_rot.tile([P, CHUNK], F32, tag="turn")
+                    for j in range(TILES):
+                        nc.tensor.transpose(turned[:, j * P:(j + 1) * P],
+                                            xh[j][:, t * P:(t + 1) * P], ident_f32[:])
+                    nc.scalar.activation(out=xn_planes[:, t, :], in_=turned[:], func=ACT.Identity,
+                                         bias=shift[:, t:t + 1], scale=gain[:, t:t + 1])
+                xn_grouped = work.tile([P, CHUNK, PACK], BF16, tag="xn_grouped", bufs=1,
+                                       align_bytes=64)
+                nc.vector.tensor_copy(out=xn_grouped[:].rearrange("p (c i) t -> p c t i", i=4),
+                                      in_=xn_planes[:].rearrange("p t (c i) -> p c t i", i=4))
+                x_codes = work.tile([P, CHUNK], U32, tag="x_codes", bufs=3, align_bytes=64)
+                x_scales = work.tile([P, CHUNK], U8, tag="x_scales", bufs=3, align_bytes=64)
+                nc.vector.quantize_mx(out=x_codes[:].bitcast(FP8X4), scales=x_scales[:],
+                                      in_=xn_grouped[:].rearrange("p r t -> p (r t)"))
+                x_mx[s] = (x_codes, x_scales)
+
+            def turn_h(s):
+                h_sb = h_tiles.pop(s)
+                h_ps = psum_rot.tile([P, HEADS, TILES, P], BF16, tag="turn")
+                for h in range(HEADS):
+                    for j in range(TILES):
+                        nc.tensor.transpose(h_ps[:, h, j, :],
+                                            h_sb[:, j, h * D_HEAD:(h + 1) * D_HEAD], ident_bf16[:])
+                h_turned = work.tile([P, HEADS, TILES, P], BF16, tag="h_turned")
+                nc.scalar.copy(out=h_turned[:], in_=h_ps[:])
+                ht_tiles[s] = h_turned
+
+            def gate_products(s):
+                x_codes, x_scales = x_mx.pop(s)
+                mx_turned = products.tile([P, BLOCKS, CHUNK], F32, tag="mx_turned")
+                for blk in range(BLOCKS):
+                    cols = slice(blk * P, (blk + 1) * P)
+                    mx_ps = psum_rot.tile([P, CHUNK], F32, tag="mx_ps")
+                    nc.tensor.matmul_mx(out=mx_ps[:],
+                                        lhsT=w_codes[:, cols].bitcast(FP8X4),
+                                        lhsT_scale=w_scales[:, cols],
+                                        rhs=x_codes[:].bitcast(FP8X4), rhs_scale=x_scales[:],
+                                        start=True, stop=True)
+                    nc.scalar.activation(out=mx_turned[:, blk, :], in_=mx_ps[:], func=ACT.Identity,
+                                         bias=gate_bias[:, blk:blk + 1], scale=1.0)
+                mt_tiles[s] = mx_turned
+
+            def gating(s, q):
+                mx_turned = mt_tiles[s]
+                h_turned = ht_tiles[s]
+                tiles = slice(q * PAIR, (q + 1) * PAIR)
+                quarters = [(jj, h) for jj in range(PAIR) for h in range(HEADS)]
+                pre = []
+                for g in range(GATES):
+                    pre_g = psum_pre.tile([P, PAIR, D_HID], F32, tag="pre%d" % g, name="pre_g")
+                    for n, (jj, h) in enumerate(quarters):
+                        j = q * PAIR + jj
+                        nc.tensor.matmul(out=pre_g[:, jj, h * D_HEAD:(h + 1) * D_HEAD],
+                                         lhsT=mx_turned[:, g * HEADS + h, j * P:(j + 1) * P],
+                                         rhs=ident_f32[:], start=(n == 0), stop=False,
+                                         is_transpose=True)
+                    for n, (jj, h) in enumerate(quarters):
+                        j = q * PAIR + jj
+                        nc.tensor.matmul(out=pre_g[:, jj, h * D_HEAD:(h + 1) * D_HEAD],
+                                         lhsT=h_turned[:, h, j, :], rhs=r_sb[:, g, h, :],
+                                         start=False, stop=(n == len(quarters) - 1))
+                    pre.append(pre_g)
+                shape = [P, PAIR, D_HID]
+                zt = work.tile(shape, F32, tag="zt")
+                nc.scalar.activation(out=zt[:], in_=pre[GZ][:], func=ACT.Tanh)
+                th = work.tile(shape, F32, tag="th")
+                nc.scalar.activation(out=th[:], in_=pre[GO][:], func=ACT.Tanh, scale=0.5)
+                fm = work.tile(shape, F32, tag="fm")
+                nc.vector.tensor_tensor(out=fm[:], in0=pre[GF][:], in1=m_tiles[s][:, tiles, :],
+                                        op=ALU.add)
+                diff = work.tile(shape, F32, tag="diff")
+                nc.vector.tensor_tensor(out=diff[:], in0=pre[GI][:], in1=fm[:], op=ALU.subtract)
+                if q == 0:
+                    m_out[s] = work.tile([P, TILES, D_HID], F32, tag="m_stage", name="m_stage")
+                    c_out[s] = work.tile([P, TILES, D_HID], F32, tag="c_stage", name="c_stage")
+                nc.vector.tensor_tensor(out=m_out[s][:, tiles, :], in0=pre[GI][:], in1=fm[:],
+                                        op=ALU.max)
+                e_i = work.tile(shape, F32, tag="e_i")
+                nc.scalar.activation(out=e_i[:], in_=diff[:], func=ACT.Exp)
+                e_f = work.tile(shape, F32, tag="e_f")
+                nc.scalar.activation(out=e_f[:], in_=diff[:], func=ACT.Exp, scale=-1.0)
+                ct = c_out[s][:, tiles, :]
+                nt = nt_keep[s][:, tiles, :]
+                iz = work.tile(shape, F32, tag="iz", bufs=1)
+                nc.vector.scalar_tensor_tensor(out=ct, in0=e_f[:], scalar=1.0,
+                                               in1=c_tiles[s][:, tiles, :],
+                                               op0=ALU.min, op1=ALU.mult)
+                nc.vector.scalar_tensor_tensor(out=nt, in0=e_f[:], scalar=1.0,
+                                               in1=n_tiles[s][:, tiles, :],
+                                               op0=ALU.min, op1=ALU.mult)
+                nc.vector.scalar_tensor_tensor(out=iz[:], in0=e_i[:], scalar=1.0, in1=zt[:],
+                                               op0=ALU.min, op1=ALU.mult)
+                nc.vector.scalar_tensor_tensor(out=nt, in0=e_i[:], scalar=1.0, in1=nt,
+                                               op0=ALU.min, op1=ALU.add)
+                nc.vector.tensor_tensor(out=ct, in0=ct, in1=iz[:], op=ALU.add)
+                nc.scalar.activation(out=sg_keep[s][:, tiles, :], in_=nt, func=ACT.Sign,
+                                     bias=div_eps[:, 0:1], scale=1.0)
+                nc.vector.scalar_tensor_tensor(out=oc_keep[s][:, tiles, :], in0=th[:], scalar=1.0,
+                                               in1=ct, op0=ALU.add, op1=ALU.mult)
+
+            def store_chunk(s):
+                nc.sync.dma_start(out=chunk_rows(out_3, s), in_=m_out.pop(s)[:])
+                nc.sync.dma_start(out=chunk_rows(out_2, s), in_=nt_keep[s][:])
+                nc.sync.dma_start(out=chunk_rows(out_1, s), in_=c_out.pop(s)[:])
+
+            normalise(0)
+            normalise(1)
+            quantise_xn(0)
+            turn_h(0)
+            gate_products(0)
+            for s in range(N_CHUNKS):
+                if s + 3 < N_CHUNKS:
+                    load_x(s + 3)
+                if s + 1 < N_CHUNKS:
+                    load_state(s + 1)
+                if s + 2 < N_CHUNKS:
+                    normalise(s + 2)
+                if s + 1 < N_CHUNKS:
+                    quantise_xn(s + 1)
+                    turn_h(s + 1)
+                    gate_products(s + 1)
+                gating(s, 0)
+                gating(s, 1)
+                store_chunk(s)
+
+        with tc.tile_pool(name="tail", bufs=3, reuse_waits="tile") as tail:
+            halves = [slice(q * PAIR, (q + 1) * PAIR) for q in range(N_PAIRS)]
+            for s in range(N_CHUNKS):
+                inv = tail.tile([P, TILES, D_HID], F32)
+                h_stage = tail.tile([P, TILES, D_HID], F32)
+                for tiles in halves:
+                    nc.scalar.activation(out=inv[:, tiles, :], in_=nt_keep[s][:, tiles, :],
+                                         func=ACT.Abs_reciprocal_sqrt, bias=div_eps[:, 0:1], scale=1.0)
+                for tiles in halves:
+                    nc.scalar.activation(out=inv[:, tiles, :], in_=inv[:, tiles, :], func=ACT.Square)
+                for tiles in halves:
+                    nc.vector.scalar_tensor_tensor(out=inv[:, tiles, :], in0=oc_keep[s][:, tiles, :],
+                                                   scalar=0.5, in1=inv[:, tiles, :],
+                                                   op0=ALU.mult, op1=ALU.mult)
+                for tiles in halves:
+                    nc.vector.tensor_tensor(out=h_stage[:, tiles, :], in0=inv[:, tiles, :],
+                                            in1=sg_keep[s][:, tiles, :], op=ALU.mult)
+                nc.sync.dma_start(out=chunk_rows(out_0, s), in_=h_stage[:])

@@ -10,6 +10,10 @@ U8 = mybir.dt.uint8
 FP8X4 = mybir.dt.float8_e4m3fn_x4
 ALU = mybir.AluOpType
 ACT = mybir.ActivationFunctionType
+PE = mybir.EngineType.PE
+SCALAR = mybir.EngineType.Activation
+VECTOR = mybir.EngineType.DVE
+GPSIMD = mybir.EngineType.Pool
 
 P = 128
 PACK = 4
@@ -28,6 +32,7 @@ CHUNK = TILES * P
 N_CHUNKS = ROWS // CHUNK
 PAIR = 2
 N_PAIRS = TILES // PAIR
+N_HALVES = N_CHUNKS * N_PAIRS
 
 FLOPS = 2 * ROWS * D_IN * GATES * D_HID + 2 * ROWS * D_HEAD * GATES * D_HID
 
@@ -54,26 +59,16 @@ def tile_slstmblock_pa_t_kernel(
         psum_pre = stack.enter_context(tc.psum_pool(name="psum_pre", bufs=1))
         psum_rot = stack.enter_context(tc.psum_pool(name="psum_rot", bufs=2))
 
+        div_eps = const.tile([P, 1], F32)
+        nc.vector.memset(div_eps[:], DIV_EPS)
+        warm = const.tile([P, 1], F32)
+        nc.scalar.activation(out=warm[:], in_=div_eps[:], func=ACT.Exp)
         ident_f32 = const.tile([P, P], F32)
         make_identity(nc, ident_f32[:])
         ident_bf16 = const.tile([P, P], BF16)
         make_identity(nc, ident_bf16[:])
         neg_half = const.tile([P, TILES], F32)
         nc.vector.memset(neg_half[:], -0.5)
-        div_eps = const.tile([P, 1], F32)
-        nc.vector.memset(div_eps[:], DIV_EPS)
-
-        vec_rows = const.tile([P, P], BF16)
-        nc.vector.memset(vec_rows[:], 0.0)
-        ln_rows = const.tile([P, 1, PACK], BF16)
-        nc.scalar.dma_start(out=ln_rows[:, 0, :], in_=ln_w.rearrange("(p t) -> p t", t=PACK))
-        ln_rows_b = const.tile([P, 1, PACK], BF16)
-        nc.scalar.dma_start(out=ln_rows_b[:, 0, :], in_=ln_b.rearrange("(p t) -> p t", t=PACK))
-        for g in range(GATES):
-            nc.scalar.dma_start(out=vec_rows[8 + HEADS * g:8 + HEADS * (g + 1), :],
-                                in_=biases[g].rearrange("(h f) -> h f", f=D_HEAD))
-            nc.scalar.dma_start(out=vec_rows[16 + HEADS * g:16 + HEADS * (g + 1), :],
-                                in_=rec_biases[g].rearrange("(h f) -> h f", f=D_HEAD))
 
         x_tiles = {}
         h_tiles = {}
@@ -86,10 +81,12 @@ def tile_slstmblock_pa_t_kernel(
             nc.sync.dma_start(out=x_sb[:], in_=chunk_rows(x, s))
             x_tiles[s] = x_sb
 
-        def load_state(s):
+        def load_h(s):
             h_sb = loads.tile([P, TILES, D_HID], BF16, tag="h_sb")
             nc.sync.dma_start(out=h_sb[:], in_=chunk_rows(h_prev, s))
             h_tiles[s] = h_sb
+
+        def load_state(s):
             m_sb = loads.tile([P, TILES, D_HID], BF16, tag="m_sb")
             nc.sync.dma_start(out=m_sb[:], in_=chunk_rows(m_prev, s))
             m_tiles[s] = m_sb
@@ -102,222 +99,435 @@ def tile_slstmblock_pa_t_kernel(
 
         load_x(0)
 
+        vec_rows = const.tile([P, P], BF16)
+        nc.vector.memset(vec_rows[:], 0.0)
+        lnw_rows = const.tile([P, PACK], BF16)
+        nc.scalar.dma_start(out=lnw_rows[:], in_=ln_w.rearrange("(p t) -> p t", t=PACK))
+        lnb_rows = const.tile([P, PACK], BF16)
+        nc.scalar.dma_start(out=lnb_rows[:], in_=ln_b.rearrange("(p t) -> p t", t=PACK))
+        for g in range(GATES):
+            nc.scalar.dma_start(out=vec_rows[8 + HEADS * g:8 + HEADS * (g + 1), :],
+                                in_=biases[g].rearrange("(h f) -> h f", f=D_HEAD))
+            nc.scalar.dma_start(out=vec_rows[16 + HEADS * g:16 + HEADS * (g + 1), :],
+                                in_=rec_biases[g].rearrange("(h f) -> h f", f=D_HEAD))
+
         w_codes = const.tile([P, GATES * D_HID], U32, align_bytes=64)
         w_scales = const.tile([P, GATES * D_HID], U8, align_bytes=64)
         r_sb = const.tile([P, GATES, HEADS, D_HEAD], BF16)
-        with tc.tile_pool(name="setup", bufs=2) as setup:
-            for g in range(GATES):
-                w_raw = setup.tile([P, PACK, D_HID], BF16)
-                nc.sync.dma_start(out=w_raw[:], in_=weights[g].rearrange("(p t) f -> p t f", t=PACK))
-                w_grouped = setup.tile([P, D_HID, PACK], BF16, align_bytes=64)
-                nc.scalar.copy(out=w_grouped[:], in_=w_raw[:].rearrange("p t f -> p f t"))
-                cols = slice(g * D_HID, (g + 1) * D_HID)
-                nc.vector.quantize_mx(
-                    out=w_codes[:, cols].bitcast(FP8X4),
-                    scales=w_scales[:, cols],
-                    in_=w_grouped[:].rearrange("p f t -> p (f t)"),
-                )
-        load_x(1)
-        load_state(0)
-        for g in range(GATES):
-            nc.sync.dma_start(out=r_sb[:, g, :, :], in_=recurrents[g].rearrange("h k f -> k h f"))
-        load_x(2)
-
-        vec_ps = psum_rot.tile([P, P], BF16, tag="turn")
-        nc.tensor.transpose(vec_ps[:], vec_rows[:], ident_bf16[:])
-        vec_cols = const.tile([P, 24], F32)
-        nc.vector.tensor_copy(out=vec_cols[:], in_=vec_ps[:, 0:24])
         ln_cols = const.tile([P, 2 * PACK], F32)
-        nc.vector.tensor_copy(out=ln_cols[:, 0:PACK], in_=ln_rows[:, 0, :])
-        nc.vector.tensor_copy(out=ln_cols[:, PACK:2 * PACK], in_=ln_rows_b[:, 0, :])
+        vec_cols = const.tile([P, 24], F32)
+        gate_bias = const.tile([P, BLOCKS], F32)
         gain = ln_cols[:, 0:PACK]
         shift = ln_cols[:, PACK:2 * PACK]
-        gate_bias = const.tile([P, BLOCKS], F32)
-        nc.vector.tensor_add(out=gate_bias[:], in0=vec_cols[:, 8:16], in1=vec_cols[:, 16:24])
 
         nt_keep = [keep.tile([P, TILES, D_HID], F32, name="nt_keep%d" % s) for s in range(N_CHUNKS)]
         oc_keep = [keep.tile([P, TILES, D_HID], F32, name="oc_keep%d" % s) for s in range(N_CHUNKS)]
         sg_keep = [keep.tile([P, TILES, D_HID], BF16, name="sg_keep%d" % s) for s in range(N_CHUNKS)]
 
-        with ExitStack() as main_stack:
-            products = main_stack.enter_context(
-                tc.tile_pool(name="products", bufs=2, reuse_waits="tile"))
-            work = main_stack.enter_context(tc.tile_pool(name="work", bufs=2, reuse_waits="tile"))
-            xh_tiles = {}
-            x_mx = {}
-            ht_tiles = {}
-            mt_tiles = {}
+        ln_pool = stack.enter_context(tc.tile_pool(name="ln_pool", bufs=2, reuse_waits="tile"))
+        stats_of = {}
+        scale_of = {}
+        xh_tiles = {}
+        planes_of = {}
+        grouped_of = {}
+        x_mx = {}
+        ht_tiles = {}
+        mt_tiles = {}
+
+        def statistics(s, j):
+            if j == 0:
+                stats_of[s] = ln_pool.tile([P, TILES, 6], F32, tag="stats", name="stats")
+            nc.vector.bn_stats(out=stats_of[s][:, j, :], in_=x_tiles[s][:, j, :])
+
+        def finish_statistics(s):
+            stats = stats_of.pop(s)
+            mean_var = ln_pool.tile([P, TILES, 2], F32, tag="mean_var")
+            for j in range(TILES):
+                nc.vector.bn_aggr(out=mean_var[:, j, :], in_=stats[:, j, :])
+            var_eps = ln_pool.tile([P, TILES], F32, tag="var_eps")
+            nc.vector.tensor_scalar_add(out=var_eps[:], in0=mean_var[:, :, 1], scalar1=LN_EPS)
+            neg_mean = ln_pool.tile([P, TILES], F32, tag="neg_mean")
+            nc.vector.tensor_scalar_mul(out=neg_mean[:], in0=mean_var[:, :, 0], scalar1=-1.0)
+            rstd = ln_pool.tile([P, TILES], F32, tag="rstd")
+            nc.gpsimd.tensor_tensor(out=rstd[:], in0=var_eps[:], in1=neg_half[:], op=ALU.pow)
+            scale_of[s] = (neg_mean, rstd)
+            xh_tiles[s] = []
+
+        def normalise(s, j, engine):
+            neg_mean, rstd = scale_of[s]
+            xh_j = ln_pool.tile([P, D_IN], F32, tag="xh", bufs=2 * TILES)
+            engine.tensor_scalar(out=xh_j[:].rearrange("p (t k) -> p t k", t=PACK),
+                                 in0=x_tiles[s][:, j, :].rearrange("p (k t) -> p t k", t=PACK),
+                                 scalar1=neg_mean[:, j:j + 1], scalar2=rstd[:, j:j + 1],
+                                 op0=ALU.add, op1=ALU.mult)
+            xh_tiles[s].append(xh_j)
+
+        def turn_x(s, t, on_vector=False):
+            if t == 0:
+                planes_of[s] = ln_pool.tile([P, PACK, CHUNK], BF16, tag="planes", bufs=1, name="planes")
+            turned = psum_rot.tile([P, CHUNK], F32, tag="turn")
+            for j in range(TILES):
+                nc.tensor.transpose(turned[:, j * P:(j + 1) * P],
+                                    xh_tiles[s][j][:, t * P:(t + 1) * P], ident_f32[:])
+            if on_vector:
+                nc.vector.tensor_scalar(out=planes_of[s][:, t, :], in0=turned[:],
+                                        scalar1=gain[:, t:t + 1], scalar2=shift[:, t:t + 1],
+                                        op0=ALU.mult, op1=ALU.add)
+            else:
+                nc.scalar.activation(out=planes_of[s][:, t, :], in_=turned[:], func=ACT.Identity,
+                                     bias=shift[:, t:t + 1], scale=gain[:, t:t + 1])
+
+        def regroup(s):
+            grouped = ln_pool.tile([P, CHUNK, PACK], BF16, tag="grouped", bufs=1, align_bytes=64)
+            nc.vector.tensor_copy(out=grouped[:].rearrange("p (c i) t -> p c t i", i=4),
+                                  in_=planes_of.pop(s)[:].rearrange("p t (c i) -> p c t i", i=4))
+            grouped_of[s] = grouped
+
+        def quantise(s):
+            x_codes = ln_pool.tile([P, CHUNK], U32, tag="x_codes", align_bytes=64)
+            x_scales = ln_pool.tile([P, CHUNK], U8, tag="x_scales", align_bytes=64)
+            nc.vector.quantize_mx(out=x_codes[:].bitcast(FP8X4), scales=x_scales[:],
+                                  in_=grouped_of.pop(s)[:].rearrange("p r t -> p (r t)"))
+            x_mx[s] = (x_codes, x_scales)
+
+        def turn_h(s):
+            h_sb = h_tiles.pop(s)
+            h_ps = psum_rot.tile([P, HEADS, TILES, P], BF16, tag="turn")
+            for h in range(HEADS):
+                for j in range(TILES):
+                    nc.tensor.transpose(h_ps[:, h, j, :],
+                                        h_sb[:, j, h * D_HEAD:(h + 1) * D_HEAD], ident_bf16[:])
+            h_turned = ln_pool.tile([P, HEADS, TILES, P], BF16, tag="h_turned")
+            nc.scalar.copy(out=h_turned[:], in_=h_ps[:])
+            ht_tiles[s] = h_turned
+
+        with tc.tile_pool(name="setup", bufs=GATES) as setup:
+            w_raw_tiles = []
+            for g in range(GATES):
+                w_raw = setup.tile([P, PACK, D_HID], BF16)
+                nc.sync.dma_start(out=w_raw[:], in_=weights[g].rearrange("(p t) f -> p t f", t=PACK))
+                w_raw_tiles.append(w_raw)
+            load_x(1)
+            load_h(0)
+            for g in range(GATES):
+                nc.sync.dma_start(out=r_sb[:, g, :, :], in_=recurrents[g].rearrange("h k f -> k h f"))
+            load_x(2)
+            load_state(0)
+            w_grouped_tiles = {}
+
+            def group_weights(g, copy):
+                w_grouped = setup.tile([P, D_HID, PACK], BF16, align_bytes=64)
+                copy(out=w_grouped[:].rearrange("p (c i) t -> p c t i", i=4),
+                     in_=w_raw_tiles[g][:].rearrange("p t (c i) -> p c t i", i=4))
+                w_grouped_tiles[g] = w_grouped
+
+            def quantise_weights(g):
+                cols = slice(g * D_HID, (g + 1) * D_HID)
+                nc.vector.quantize_mx(out=w_codes[:, cols].bitcast(FP8X4), scales=w_scales[:, cols],
+                                      in_=w_grouped_tiles[g][:].rearrange("p f t -> p (f t)"))
+
+            with ExitStack():
+                nc.gpsimd.tensor_copy(out=ln_cols[:, 0:PACK], in_=lnw_rows[:])
+                nc.gpsimd.tensor_copy(out=ln_cols[:, PACK:2 * PACK], in_=lnb_rows[:])
+                for j in range(TILES):
+                    statistics(0, j)
+                finish_statistics(0)
+                group_weights(GF, nc.scalar.copy)
+                group_weights(GZ, nc.vector.tensor_copy)
+                group_weights(GO, nc.scalar.copy)
+                group_weights(GI, nc.vector.tensor_copy)
+                vec_ps = psum_rot.tile([P, P], BF16, tag="turn")
+                nc.tensor.transpose(vec_ps[:], vec_rows[:], ident_bf16[:])
+                nc.scalar.copy(out=vec_cols[:], in_=vec_ps[:, 0:24])
+                nc.gpsimd.tensor_tensor(out=gate_bias[:], in0=vec_cols[:, 8:16],
+                                        in1=vec_cols[:, 16:24], op=ALU.add)
+                quantise_weights(GZ)
+                quantise_weights(GF)
+                for j in range(TILES):
+                    normalise(0, j, nc.vector)
+                turn_x(0, 0)
+                quantise_weights(GI)
+                quantise_weights(GO)
+                statistics(1, 0)
+                turn_x(0, 1, on_vector=True)
+                turn_x(0, 2)
+                statistics(1, 1)
+                turn_x(0, 3, on_vector=True)
+                statistics(1, 2)
+                regroup(0)
+                statistics(1, 3)
+                quantise(0)
+                finish_statistics(1)
+                for j in range(TILES):
+                    normalise(1, j, nc.gpsimd)
+                turn_h(0)
+                load_x(3)
+
+        with ExitStack():
+            gate = stack.enter_context(tc.tile_pool(name="gate", bufs=2, reuse_waits="tile"))
+
+            def gate_product(s, blk, on_vector=False):
+                x_codes, x_scales = x_mx[s]
+                if s not in mt_tiles:
+                    mt_tiles[s] = gate.tile([P, BLOCKS, CHUNK], F32, tag="mx_turned",
+                                            name="mx_turned")
+                cols = slice(blk * P, (blk + 1) * P)
+                mx_ps = psum_rot.tile([P, CHUNK], F32, tag="mx_ps")
+                nc.tensor.matmul_mx(out=mx_ps[:],
+                                    lhsT=w_codes[:, cols].bitcast(FP8X4),
+                                    lhsT_scale=w_scales[:, cols],
+                                    rhs=x_codes[:].bitcast(FP8X4), rhs_scale=x_scales[:],
+                                    start=True, stop=True)
+                if on_vector:
+                    nc.vector.tensor_scalar_add(out=mt_tiles[s][:, blk, :], in0=mx_ps[:],
+                                                scalar1=gate_bias[:, blk:blk + 1])
+                else:
+                    nc.scalar.activation(out=mt_tiles[s][:, blk, :], in_=mx_ps[:], func=ACT.Identity,
+                                         bias=gate_bias[:, blk:blk + 1], scale=1.0)
+
+            shape = [P, PAIR, D_HID]
+            pre_of = {}
+            fm_of = {}
+            d_of = {}
+            zt_of = {}
+            th_of = {}
+            ei_of = {}
+            ef_of = {}
+            iz_of = {}
             m_out = {}
             c_out = {}
 
-            def normalise(s):
-                x_sb = x_tiles.pop(s)
-                stats = work.tile([P, TILES, 6], F32, tag="stats")
-                mean_var = work.tile([P, TILES, 2], F32, tag="mean_var")
-                for j in range(TILES):
-                    nc.vector.bn_stats(out=stats[:, j, :], in_=x_sb[:, j, :])
-                for j in range(TILES):
-                    nc.vector.bn_aggr(out=mean_var[:, j, :], in_=stats[:, j, :])
-                var_eps = work.tile([P, TILES], F32, tag="var_eps")
-                nc.vector.tensor_scalar_add(out=var_eps[:], in0=mean_var[:, :, 1], scalar1=LN_EPS)
-                neg_mean = work.tile([P, TILES], F32, tag="neg_mean")
-                nc.vector.tensor_scalar_mul(out=neg_mean[:], in0=mean_var[:, :, 0], scalar1=-1.0)
-                rstd = work.tile([P, TILES], F32, tag="rstd")
-                nc.gpsimd.tensor_tensor(out=rstd[:], in0=var_eps[:], in1=neg_half[:], op=ALU.pow)
-                xh = []
-                for j in range(TILES):
-                    xh_j = work.tile([P, D_IN], F32, tag="xh", bufs=2 * TILES)
-                    nc.gpsimd.tensor_scalar(out=xh_j[:].rearrange("p (t k) -> p t k", t=PACK),
-                                            in0=x_sb[:, j, :].rearrange("p (k t) -> p t k", t=PACK),
-                                            scalar1=neg_mean[:, j:j + 1], scalar2=rstd[:, j:j + 1],
-                                            op0=ALU.add, op1=ALU.mult)
-                    xh.append(xh_j)
-                xh_tiles[s] = xh
+            def tiles_of(i):
+                q = i % N_PAIRS
+                return i // N_PAIRS, slice(q * PAIR, (q + 1) * PAIR)
 
-            def quantise_xn(s):
-                xh = xh_tiles.pop(s)
-                xn_planes = work.tile([P, PACK, CHUNK], BF16, tag="xn_planes", bufs=1)
-                for t in range(PACK):
-                    turned = psum_rot.tile([P, CHUNK], F32, tag="turn")
-                    for j in range(TILES):
-                        nc.tensor.transpose(turned[:, j * P:(j + 1) * P],
-                                            xh[j][:, t * P:(t + 1) * P], ident_f32[:])
-                    nc.scalar.activation(out=xn_planes[:, t, :], in_=turned[:], func=ACT.Identity,
-                                         bias=shift[:, t:t + 1], scale=gain[:, t:t + 1])
-                xn_grouped = work.tile([P, CHUNK, PACK], BF16, tag="xn_grouped", bufs=1,
-                                       align_bytes=64)
-                nc.vector.tensor_copy(out=xn_grouped[:].rearrange("p (c i) t -> p c t i", i=4),
-                                      in_=xn_planes[:].rearrange("p t (c i) -> p c t i", i=4))
-                x_codes = work.tile([P, CHUNK], U32, tag="x_codes", bufs=3, align_bytes=64)
-                x_scales = work.tile([P, CHUNK], U8, tag="x_scales", bufs=3, align_bytes=64)
-                nc.vector.quantize_mx(out=x_codes[:].bitcast(FP8X4), scales=x_scales[:],
-                                      in_=xn_grouped[:].rearrange("p r t -> p (r t)"))
-                x_mx[s] = (x_codes, x_scales)
-
-            def turn_h(s):
-                h_sb = h_tiles.pop(s)
-                h_ps = psum_rot.tile([P, HEADS, TILES, P], BF16, tag="turn")
-                for h in range(HEADS):
-                    for j in range(TILES):
-                        nc.tensor.transpose(h_ps[:, h, j, :],
-                                            h_sb[:, j, h * D_HEAD:(h + 1) * D_HEAD], ident_bf16[:])
-                h_turned = work.tile([P, HEADS, TILES, P], BF16, tag="h_turned")
-                nc.scalar.copy(out=h_turned[:], in_=h_ps[:])
-                ht_tiles[s] = h_turned
-
-            def gate_products(s):
-                x_codes, x_scales = x_mx.pop(s)
-                mx_turned = products.tile([P, BLOCKS, CHUNK], F32, tag="mx_turned")
-                for blk in range(BLOCKS):
-                    cols = slice(blk * P, (blk + 1) * P)
-                    mx_ps = psum_rot.tile([P, CHUNK], F32, tag="mx_ps")
-                    nc.tensor.matmul_mx(out=mx_ps[:],
-                                        lhsT=w_codes[:, cols].bitcast(FP8X4),
-                                        lhsT_scale=w_scales[:, cols],
-                                        rhs=x_codes[:].bitcast(FP8X4), rhs_scale=x_scales[:],
-                                        start=True, stop=True)
-                    nc.scalar.activation(out=mx_turned[:, blk, :], in_=mx_ps[:], func=ACT.Identity,
-                                         bias=gate_bias[:, blk:blk + 1], scale=1.0)
-                mt_tiles[s] = mx_turned
-
-            def gating(s, q):
-                mx_turned = mt_tiles[s]
-                h_turned = ht_tiles[s]
-                tiles = slice(q * PAIR, (q + 1) * PAIR)
+            def fill(i, g):
+                s, q = i // N_PAIRS, i % N_PAIRS
                 quarters = [(jj, h) for jj in range(PAIR) for h in range(HEADS)]
-                pre = []
-                for g in range(GATES):
-                    pre_g = psum_pre.tile([P, PAIR, D_HID], F32, tag="pre%d" % g, name="pre_g")
-                    for n, (jj, h) in enumerate(quarters):
-                        j = q * PAIR + jj
-                        nc.tensor.matmul(out=pre_g[:, jj, h * D_HEAD:(h + 1) * D_HEAD],
-                                         lhsT=mx_turned[:, g * HEADS + h, j * P:(j + 1) * P],
-                                         rhs=ident_f32[:], start=(n == 0), stop=False,
-                                         is_transpose=True)
-                    for n, (jj, h) in enumerate(quarters):
-                        j = q * PAIR + jj
-                        nc.tensor.matmul(out=pre_g[:, jj, h * D_HEAD:(h + 1) * D_HEAD],
-                                         lhsT=h_turned[:, h, j, :], rhs=r_sb[:, g, h, :],
-                                         start=False, stop=(n == len(quarters) - 1))
-                    pre.append(pre_g)
-                shape = [P, PAIR, D_HID]
-                zt = work.tile(shape, F32, tag="zt")
-                nc.scalar.activation(out=zt[:], in_=pre[GZ][:], func=ACT.Tanh)
-                th = work.tile(shape, F32, tag="th")
-                nc.scalar.activation(out=th[:], in_=pre[GO][:], func=ACT.Tanh, scale=0.5)
-                fm = work.tile(shape, F32, tag="fm")
-                nc.vector.tensor_tensor(out=fm[:], in0=pre[GF][:], in1=m_tiles[s][:, tiles, :],
-                                        op=ALU.add)
-                diff = work.tile(shape, F32, tag="diff")
-                nc.vector.tensor_tensor(out=diff[:], in0=pre[GI][:], in1=fm[:], op=ALU.subtract)
-                if q == 0:
-                    m_out[s] = work.tile([P, TILES, D_HID], F32, tag="m_stage", name="m_stage")
-                    c_out[s] = work.tile([P, TILES, D_HID], F32, tag="c_stage", name="c_stage")
-                nc.vector.tensor_tensor(out=m_out[s][:, tiles, :], in0=pre[GI][:], in1=fm[:],
-                                        op=ALU.max)
-                e_i = work.tile(shape, F32, tag="e_i")
-                nc.scalar.activation(out=e_i[:], in_=diff[:], func=ACT.Exp)
-                e_f = work.tile(shape, F32, tag="e_f")
-                nc.scalar.activation(out=e_f[:], in_=diff[:], func=ACT.Exp, scale=-1.0)
-                ct = c_out[s][:, tiles, :]
-                nt = nt_keep[s][:, tiles, :]
-                iz = work.tile(shape, F32, tag="iz", bufs=1)
-                nc.vector.scalar_tensor_tensor(out=ct, in0=e_f[:], scalar=1.0,
+                pre_g = psum_pre.tile(shape, F32, tag="pre%d" % g, name="pre_g")
+                for n, (jj, h) in enumerate(quarters):
+                    j = q * PAIR + jj
+                    nc.tensor.matmul(out=pre_g[:, jj, h * D_HEAD:(h + 1) * D_HEAD],
+                                     lhsT=mt_tiles[s][:, g * HEADS + h, j * P:(j + 1) * P],
+                                     rhs=ident_f32[:], start=(n == 0), stop=False,
+                                     is_transpose=True)
+                for n, (jj, h) in enumerate(quarters):
+                    j = q * PAIR + jj
+                    nc.tensor.matmul(out=pre_g[:, jj, h * D_HEAD:(h + 1) * D_HEAD],
+                                     lhsT=ht_tiles[s][:, h, j, :], rhs=r_sb[:, g, h, :],
+                                     start=False, stop=(g != GF and n == len(quarters) - 1))
+                if g == GF:
+                    nc.tensor.matmul(out=pre_g[:], lhsT=ident_bf16[:],
+                                     rhs=m_tiles[s][:, q * PAIR:(q + 1) * PAIR, :],
+                                     start=False, stop=True)
+                pre_of[i, g] = pre_g
+
+            def tanhs(i):
+                zt = gate.tile(shape, F32, tag="zt", bufs=3)
+                nc.scalar.activation(out=zt[:], in_=pre_of[i, GZ][:], func=ACT.Tanh)
+                th = gate.tile(shape, F32, tag="th", bufs=4)
+                nc.scalar.activation(out=th[:], in_=pre_of[i, GO][:], func=ACT.Tanh, scale=0.5)
+                zt_of[i] = zt
+                th_of[i] = th
+
+            def copy_fm(i):
+                fm = gate.tile(shape, F32, tag="fm")
+                nc.scalar.copy(out=fm[:], in_=pre_of[i, GF][:])
+                fm_of[i] = fm
+
+            def difference(i):
+                d = gate.tile(shape, F32, tag="d")
+                nc.vector.tensor_tensor(out=d[:], in0=pre_of[i, GI][:], in1=fm_of[i][:],
+                                        op=ALU.subtract)
+                d_of[i] = d
+
+            def maximum(i):
+                s, tiles = tiles_of(i)
+                if i % N_PAIRS == 0:
+                    m_out[s] = gate.tile([P, TILES, D_HID], F32, tag="m_stage", name="m_stage")
+                nc.vector.tensor_tensor(out=m_out[s][:, tiles, :], in0=pre_of[i, GI][:],
+                                        in1=fm_of.pop(i)[:], op=ALU.max)
+
+            def exps(i):
+                e_f = gate.tile(shape, F32, tag="e_f")
+                nc.scalar.activation(out=e_f[:], in_=d_of[i][:], func=ACT.Exp, scale=-1.0)
+                e_i = gate.tile(shape, F32, tag="e_i")
+                nc.scalar.activation(out=e_i[:], in_=d_of.pop(i)[:], func=ACT.Exp)
+                ei_of[i] = e_i
+                ef_of[i] = e_f
+
+            def c_first(i):
+                s, tiles = tiles_of(i)
+                if i % N_PAIRS == 0:
+                    c_out[s] = gate.tile([P, TILES, D_HID], F32, tag="c_stage", name="c_stage")
+                nc.vector.scalar_tensor_tensor(out=c_out[s][:, tiles, :], in0=ef_of[i][:], scalar=1.0,
                                                in1=c_tiles[s][:, tiles, :],
                                                op0=ALU.min, op1=ALU.mult)
-                nc.vector.scalar_tensor_tensor(out=nt, in0=e_f[:], scalar=1.0,
-                                               in1=n_tiles[s][:, tiles, :],
+
+            def n_first(i):
+                s, tiles = tiles_of(i)
+                nc.vector.scalar_tensor_tensor(out=nt_keep[s][:, tiles, :], in0=ef_of.pop(i)[:],
+                                               scalar=1.0, in1=n_tiles[s][:, tiles, :],
                                                op0=ALU.min, op1=ALU.mult)
-                nc.vector.scalar_tensor_tensor(out=iz[:], in0=e_i[:], scalar=1.0, in1=zt[:],
-                                               op0=ALU.min, op1=ALU.mult)
-                nc.vector.scalar_tensor_tensor(out=nt, in0=e_i[:], scalar=1.0, in1=nt,
+
+            def n_last(i):
+                s, tiles = tiles_of(i)
+                nt = nt_keep[s][:, tiles, :]
+                nc.vector.scalar_tensor_tensor(out=nt, in0=ei_of[i][:], scalar=1.0, in1=nt,
                                                op0=ALU.min, op1=ALU.add)
-                nc.vector.tensor_tensor(out=ct, in0=ct, in1=iz[:], op=ALU.add)
-                nc.scalar.activation(out=sg_keep[s][:, tiles, :], in_=nt, func=ACT.Sign,
-                                     bias=div_eps[:, 0:1], scale=1.0)
-                nc.vector.scalar_tensor_tensor(out=oc_keep[s][:, tiles, :], in0=th[:], scalar=1.0,
-                                               in1=ct, op0=ALU.add, op1=ALU.mult)
 
-            def store_chunk(s):
-                nc.sync.dma_start(out=chunk_rows(out_3, s), in_=m_out.pop(s)[:])
-                nc.sync.dma_start(out=chunk_rows(out_2, s), in_=nt_keep[s][:])
-                nc.sync.dma_start(out=chunk_rows(out_1, s), in_=c_out.pop(s)[:])
+            def i_times_z(i):
+                iz = gate.tile(shape, F32, tag="iz")
+                nc.vector.scalar_tensor_tensor(out=iz[:], in0=ei_of.pop(i)[:], scalar=1.0,
+                                               in1=zt_of.pop(i)[:], op0=ALU.min, op1=ALU.mult)
+                iz_of[i] = iz
 
-            normalise(0)
-            normalise(1)
-            quantise_xn(0)
-            turn_h(0)
-            gate_products(0)
-            for s in range(N_CHUNKS):
-                if s + 3 < N_CHUNKS:
-                    load_x(s + 3)
+            def c_last(i):
+                s, tiles = tiles_of(i)
+                ct = c_out[s][:, tiles, :]
+                nc.gpsimd.tensor_tensor(out=ct, in0=ct, in1=iz_of.pop(i)[:], op=ALU.add)
+
+            def o_times_c(i):
+                s, tiles = tiles_of(i)
+                nc.vector.scalar_tensor_tensor(out=oc_keep[s][:, tiles, :], in0=th_of.pop(i)[:],
+                                               scalar=1.0, in1=c_out[s][:, tiles, :],
+                                               op0=ALU.add, op1=ALU.mult)
+
+            def half_sign(i):
+                s, tiles = tiles_of(i)
+                nc.vector.tensor_scalar(out=sg_keep[s][:, tiles, :], in0=nt_keep[s][:, tiles, :],
+                                        scalar1=-DIV_EPS, scalar2=0.5,
+                                        op0=ALU.is_ge, op1=ALU.subtract)
+
+            order = (GF, GZ, GI, GO)
+            for n, g in enumerate(order):
+                gate_product(0, HEADS * g)
+                gate_product(0, HEADS * g + 1, on_vector=True)
+                if n >= 1:
+                    fill(0, order[n - 1])
+            fill(0, order[-1])
+            for j in range(TILES):
+                statistics(2, j)
+            finish_statistics(2)
+            load_x(4)
+            statistics(3, 0)
+            statistics(3, 1)
+
+            def half(i):
+                s, q = i // N_PAIRS, i % N_PAIRS
+                if q == 0:
+                    if s + 1 < N_CHUNKS:
+                        load_h(s + 1)
+                        load_state(s + 1)
+                elif s + 5 < N_CHUNKS:
+                    load_x(s + 5)
+                copy_fm(i)
+                tanhs(i)
+                if i >= 2:
+                    c_last(i - 2)
+                ahead = s + 2 + q
+                later = s + 3 + q
+                first = PAIR * (1 - q)
+                if ahead < N_CHUNKS:
+                    if i == 0:
+                        normalise(2, 0, nc.gpsimd)
+                        normalise(2, 1, nc.gpsimd)
+                    normalise(ahead, first, nc.gpsimd)
+                    normalise(ahead, first + 1, nc.gpsimd)
+                if q == 1 and s + 1 < N_CHUNKS:
+                    gate_product(s + 1, HEADS * GI)
+                    gate_product(s + 1, HEADS * GI + 1)
+                difference(i)
+                exps(i)
+                if i == 0:
+                    for t in range(PACK):
+                        turn_x(1, t)
+                if later < N_CHUNKS:
+                    statistics(later, first)
+                maximum(i)
+                if later < N_CHUNKS:
+                    statistics(later, first + 1)
+                if i == 0:
+                    regroup(1)
+                if i + 1 < N_HALVES:
+                    fill(i + 1, GF)
+                    fill(i + 1, GZ)
                 if s + 1 < N_CHUNKS:
-                    load_state(s + 1)
+                    if q == 0:
+                        quantise(s + 1)
+                        for g in (GF, GZ):
+                            gate_product(s + 1, HEADS * g)
+                            gate_product(s + 1, HEADS * g + 1)
+                        turn_h(s + 1)
+                    else:
+                        gate_product(s + 1, HEADS * GO)
+                        gate_product(s + 1, HEADS * GO + 1)
+                if i + 1 < N_HALVES:
+                    fill(i + 1, GI)
+                    fill(i + 1, GO)
                 if s + 2 < N_CHUNKS:
-                    normalise(s + 2)
-                if s + 1 < N_CHUNKS:
-                    quantise_xn(s + 1)
-                    turn_h(s + 1)
-                    gate_products(s + 1)
-                gating(s, 0)
-                gating(s, 1)
-                store_chunk(s)
+                    turn_x(s + 2, PAIR * q)
+                    turn_x(s + 2, PAIR * q + 1)
+                if i >= 1:
+                    c_first(i - 1)
+                    n_first(i - 1)
+                if i >= 2:
+                    o_times_c(i - 2)
+                if i >= 1:
+                    n_last(i - 1)
+                if i >= 2:
+                    half_sign(i - 2)
+                if i >= 1:
+                    i_times_z(i - 1)
+                if q == 0:
+                    if later < N_CHUNKS:
+                        finish_statistics(later)
+                    if s >= 1:
+                        nc.sync.dma_start(out=chunk_rows(out_2, s - 1), in_=nt_keep[s - 1][:])
+                else:
+                    if s + 2 < N_CHUNKS:
+                        regroup(s + 2)
+                    nc.sync.dma_start(out=chunk_rows(out_3, s), in_=m_out.pop(s)[:])
+                    if s >= 1:
+                        nc.sync.dma_start(out=chunk_rows(out_1, s - 1), in_=c_out.pop(s - 1)[:])
 
-        with tc.tile_pool(name="tail", bufs=3, reuse_waits="tile") as tail:
+            for i in range(N_HALVES - 2):
+                half(i)
+            stack.enter_context(tc.manual_schedule(engines={SCALAR}))
+            half(N_HALVES - 2)
+            half(N_HALVES - 1)
+
             halves = [slice(q * PAIR, (q + 1) * PAIR) for q in range(N_PAIRS)]
+            last = N_CHUNKS - 1
+            final = N_HALVES - 1
+            c_last(final - 1)
+            c_first(final)
+            n_first(final)
+            o_times_c(final - 1)
+            n_last(final)
+            half_sign(final - 1)
+            i_times_z(final)
+            nc.sync.dma_start(out=chunk_rows(out_2, last), in_=nt_keep[last][:])
+            c_last(final)
+            nc.sync.dma_start(out=chunk_rows(out_1, last), in_=c_out[last][:])
             for s in range(N_CHUNKS):
-                inv = tail.tile([P, TILES, D_HID], F32)
-                h_stage = tail.tile([P, TILES, D_HID], F32)
+                if s == 1:
+                    half_sign(final)
+                    o_times_c(final)
                 for tiles in halves:
-                    nc.scalar.activation(out=inv[:, tiles, :], in_=nt_keep[s][:, tiles, :],
+                    nc.scalar.activation(out=nt_keep[s][:, tiles, :], in_=nt_keep[s][:, tiles, :],
                                          func=ACT.Abs_reciprocal_sqrt, bias=div_eps[:, 0:1], scale=1.0)
                 for tiles in halves:
-                    nc.scalar.activation(out=inv[:, tiles, :], in_=inv[:, tiles, :], func=ACT.Square)
+                    nc.scalar.activation(out=nt_keep[s][:, tiles, :], in_=nt_keep[s][:, tiles, :],
+                                         func=ACT.Square)
                 for tiles in halves:
-                    nc.vector.scalar_tensor_tensor(out=inv[:, tiles, :], in0=oc_keep[s][:, tiles, :],
-                                                   scalar=0.5, in1=inv[:, tiles, :],
-                                                   op0=ALU.mult, op1=ALU.mult)
+                    nc.vector.tensor_tensor(out=oc_keep[s][:, tiles, :], in0=oc_keep[s][:, tiles, :],
+                                            in1=nt_keep[s][:, tiles, :], op=ALU.mult)
                 for tiles in halves:
-                    nc.vector.tensor_tensor(out=h_stage[:, tiles, :], in0=inv[:, tiles, :],
+                    nc.vector.tensor_tensor(out=oc_keep[s][:, tiles, :], in0=oc_keep[s][:, tiles, :],
                                             in1=sg_keep[s][:, tiles, :], op=ALU.mult)
-                nc.sync.dma_start(out=chunk_rows(out_0, s), in_=h_stage[:])
+                    if s == last:
+                        nc.sync.dma_start(out=chunk_rows(out_0, s)[:, tiles, :],
+                                          in_=oc_keep[s][:, tiles, :])
+                if s < last:
+                    nc.sync.dma_start(out=chunk_rows(out_0, s), in_=oc_keep[s][:])

@@ -259,7 +259,7 @@ def tile_slstmblock_pa_t_kernel(
                 quantise(0)
                 finish_statistics(1)
                 for j in range(TILES):
-                    normalise(1, j, nc.gpsimd)
+                    normalise(1, j, nc.vector)
                 turn_h(0)
                 load_x(3)
 
@@ -385,7 +385,7 @@ def tile_slstmblock_pa_t_kernel(
             def c_last(i):
                 s, tiles = tiles_of(i)
                 ct = c_out[s][:, tiles, :]
-                nc.gpsimd.tensor_tensor(out=ct, in0=ct, in1=iz_of.pop(i)[:], op=ALU.add)
+                nc.vector.tensor_tensor(out=ct, in0=ct, in1=iz_of.pop(i)[:], op=ALU.add)
 
             def o_times_c(i):
                 s, tiles = tiles_of(i)
@@ -430,10 +430,10 @@ def tile_slstmblock_pa_t_kernel(
                 first = PAIR * (1 - q)
                 if ahead < N_CHUNKS:
                     if i == 0:
-                        normalise(2, 0, nc.gpsimd)
-                        normalise(2, 1, nc.gpsimd)
-                    normalise(ahead, first, nc.gpsimd)
-                    normalise(ahead, first + 1, nc.gpsimd)
+                        normalise(2, 0, nc.vector)
+                        normalise(2, 1, nc.vector)
+                    normalise(ahead, first, nc.vector)
+                    normalise(ahead, first + 1, nc.vector)
                 if q == 1 and s + 1 < N_CHUNKS:
                     gate_product(s + 1, HEADS * GI)
                     gate_product(s + 1, HEADS * GI + 1)

@@ -145,9 +145,9 @@ def tile_slstmblock_pa_t_kernel(
             for j in range(TILES):
                 nc.vector.bn_aggr(out=mean_var[:, j, :], in_=stats[:, j, :])
             var_eps = ln_pool.tile([P, TILES], F32, tag="var_eps")
-            nc.vector.tensor_scalar_add(out=var_eps[:], in0=mean_var[:, :, 1], scalar1=LN_EPS)
+            nc.gpsimd.tensor_scalar_add(out=var_eps[:], in0=mean_var[:, :, 1], scalar1=LN_EPS)
             neg_mean = ln_pool.tile([P, TILES], F32, tag="neg_mean")
-            nc.vector.tensor_scalar_mul(out=neg_mean[:], in0=mean_var[:, :, 0], scalar1=-1.0)
+            nc.gpsimd.tensor_scalar_mul(out=neg_mean[:], in0=mean_var[:, :, 0], scalar1=-1.0)
             rstd = ln_pool.tile([P, TILES], F32, tag="rstd")
             nc.gpsimd.tensor_tensor(out=rstd[:], in0=var_eps[:], in1=neg_half[:], op=ALU.pow)
             scale_of[s] = (neg_mean, rstd)
@@ -198,7 +198,7 @@ def tile_slstmblock_pa_t_kernel(
                     nc.tensor.transpose(h_ps[:, h, j, :],
                                         h_sb[:, j, h * D_HEAD:(h + 1) * D_HEAD], ident_bf16[:])
             h_turned = ln_pool.tile([P, HEADS, TILES, P], BF16, tag="h_turned")
-            nc.scalar.copy(out=h_turned[:], in_=h_ps[:])
+            nc.vector.tensor_copy(out=h_turned[:], in_=h_ps[:])
             ht_tiles[s] = h_turned
 
         with tc.tile_pool(name="setup", bufs=GATES) as setup:
@@ -233,9 +233,9 @@ def tile_slstmblock_pa_t_kernel(
                     statistics(0, j)
                 finish_statistics(0)
                 group_weights(GF, nc.scalar.copy)
-                group_weights(GZ, nc.vector.tensor_copy)
+                group_weights(GZ, nc.scalar.copy)
                 group_weights(GO, nc.scalar.copy)
-                group_weights(GI, nc.vector.tensor_copy)
+                group_weights(GI, nc.scalar.copy)
                 vec_ps = psum_rot.tile([P, P], BF16, tag="turn")
                 nc.tensor.transpose(vec_ps[:], vec_rows[:], ident_bf16[:])
                 nc.scalar.copy(out=vec_cols[:], in_=vec_ps[:, 0:24])
@@ -249,17 +249,17 @@ def tile_slstmblock_pa_t_kernel(
                 quantise_weights(GI)
                 quantise_weights(GO)
                 statistics(1, 0)
-                turn_x(0, 1, on_vector=True)
+                turn_x(0, 1)
                 turn_x(0, 2)
                 statistics(1, 1)
-                turn_x(0, 3, on_vector=True)
+                turn_x(0, 3)
                 statistics(1, 2)
                 regroup(0)
                 statistics(1, 3)
                 quantise(0)
                 finish_statistics(1)
                 for j in range(TILES):
-                    normalise(1, j, nc.vector)
+                    normalise(1, j, nc.gpsimd)
                 turn_h(0)
                 load_x(3)
 
@@ -402,7 +402,7 @@ def tile_slstmblock_pa_t_kernel(
             order = (GF, GZ, GI, GO)
             for n, g in enumerate(order):
                 gate_product(0, HEADS * g)
-                gate_product(0, HEADS * g + 1, on_vector=True)
+                gate_product(0, HEADS * g + 1)
                 if n >= 1:
                     fill(0, order[n - 1])
             fill(0, order[-1])
@@ -421,53 +421,60 @@ def tile_slstmblock_pa_t_kernel(
                         load_state(s + 1)
                 elif s + 5 < N_CHUNKS:
                     load_x(s + 5)
-                copy_fm(i)
-                tanhs(i)
-                if i >= 2:
-                    c_last(i - 2)
+                more = s + 1 < N_CHUNKS
+                nxt = i + 1 < N_HALVES
+                pairs = (GF, GZ) if q == 0 else (GI, GO)
                 ahead = s + 2 + q
                 later = s + 3 + q
                 first = PAIR * (1 - q)
-                if ahead < N_CHUNKS:
-                    if i == 0:
-                        normalise(2, 0, nc.vector)
-                        normalise(2, 1, nc.vector)
-                    normalise(ahead, first, nc.vector)
-                    normalise(ahead, first + 1, nc.vector)
-                if q == 1 and s + 1 < N_CHUNKS:
-                    gate_product(s + 1, HEADS * GI)
-                    gate_product(s + 1, HEADS * GI + 1)
-                difference(i)
-                exps(i)
                 if i == 0:
                     for t in range(PACK):
                         turn_x(1, t)
-                if later < N_CHUNKS:
-                    statistics(later, first)
-                maximum(i)
-                if later < N_CHUNKS:
-                    statistics(later, first + 1)
-                if i == 0:
                     regroup(1)
-                if i + 1 < N_HALVES:
+                copy_fm(i)
+                tanhs(i)
+                if q == 0 and more:
+                    quantise(s + 1)
+                difference(i)
+                exps(i)
+                maximum(i)
+                if ahead < N_CHUNKS:
+                    if i == 0:
+                        normalise(2, 0, nc.gpsimd)
+                        normalise(2, 1, nc.gpsimd)
+                    normalise(ahead, first, nc.gpsimd)
+                    normalise(ahead, first + 1, nc.gpsimd)
+                if nxt:
                     fill(i + 1, GF)
+                if more:
+                    gate_product(s + 1, HEADS * pairs[0])
+                if nxt:
                     fill(i + 1, GZ)
-                if s + 1 < N_CHUNKS:
-                    if q == 0:
-                        quantise(s + 1)
-                        for g in (GF, GZ):
-                            gate_product(s + 1, HEADS * g)
-                            gate_product(s + 1, HEADS * g + 1)
-                        turn_h(s + 1)
-                    else:
-                        gate_product(s + 1, HEADS * GO)
-                        gate_product(s + 1, HEADS * GO + 1)
-                if i + 1 < N_HALVES:
-                    fill(i + 1, GI)
-                    fill(i + 1, GO)
+                if more:
+                    gate_product(s + 1, HEADS * pairs[0] + 1)
                 if s + 2 < N_CHUNKS:
                     turn_x(s + 2, PAIR * q)
+                if q == 0 and nxt:
+                    fill(i + 1, GI)
+                if more:
+                    gate_product(s + 1, HEADS * pairs[1])
+                if q == 0 and more:
+                    turn_h(s + 1)
+                if q == 1 and nxt:
+                    fill(i + 1, GI)
+                if more:
+                    gate_product(s + 1, HEADS * pairs[1] + 1)
+                if q == 0 and nxt:
+                    fill(i + 1, GO)
+                if s + 2 < N_CHUNKS:
                     turn_x(s + 2, PAIR * q + 1)
+                if q == 1 and nxt:
+                    fill(i + 1, GO)
+                if i >= 2:
+                    c_last(i - 2)
+                if later < N_CHUNKS:
+                    statistics(later, first)
+                    statistics(later, first + 1)
                 if i >= 1:
                     c_first(i - 1)
                     n_first(i - 1)

@@ -198,7 +198,7 @@ def tile_slstmblock_pa_t_kernel(
                     nc.tensor.transpose(h_ps[:, h, j, :],
                                         h_sb[:, j, h * D_HEAD:(h + 1) * D_HEAD], ident_bf16[:])
             h_turned = ln_pool.tile([P, HEADS, TILES, P], BF16, tag="h_turned")
-            nc.vector.tensor_copy(out=h_turned[:], in_=h_ps[:])
+            nc.scalar.copy(out=h_turned[:], in_=h_ps[:])
             ht_tiles[s] = h_turned
 
         with tc.tile_pool(name="setup", bufs=GATES) as setup:
@@ -315,11 +315,7 @@ def tile_slstmblock_pa_t_kernel(
                     j = q * PAIR + jj
                     nc.tensor.matmul(out=pre_g[:, jj, h * D_HEAD:(h + 1) * D_HEAD],
                                      lhsT=ht_tiles[s][:, h, j, :], rhs=r_sb[:, g, h, :],
-                                     start=False, stop=(g != GF and n == len(quarters) - 1))
-                if g == GF:
-                    nc.tensor.matmul(out=pre_g[:], lhsT=ident_bf16[:],
-                                     rhs=m_tiles[s][:, q * PAIR:(q + 1) * PAIR, :],
-                                     start=False, stop=True)
+                                     start=False, stop=(n == len(quarters) - 1))
                 pre_of[i, g] = pre_g
 
             def tanhs(i):
@@ -331,8 +327,10 @@ def tile_slstmblock_pa_t_kernel(
                 th_of[i] = th
 
             def copy_fm(i):
+                s, tiles = tiles_of(i)
                 fm = gate.tile(shape, F32, tag="fm")
-                nc.scalar.copy(out=fm[:], in_=pre_of[i, GF][:])
+                nc.vector.tensor_tensor(out=fm[:], in0=pre_of[i, GF][:], in1=m_tiles[s][:, tiles, :],
+                                        op=ALU.add)
                 fm_of[i] = fm
 
             def difference(i):
@@ -395,9 +393,13 @@ def tile_slstmblock_pa_t_kernel(
 
             def half_sign(i):
                 s, tiles = tiles_of(i)
-                nc.vector.tensor_scalar(out=sg_keep[s][:, tiles, :], in0=nt_keep[s][:, tiles, :],
-                                        scalar1=-DIV_EPS, scalar2=0.5,
-                                        op0=ALU.is_ge, op1=ALU.subtract)
+                if i % N_PAIRS == 0:
+                    nc.scalar.activation(out=sg_keep[s][:, tiles, :], in_=nt_keep[s][:, tiles, :],
+                                         func=ACT.Sign, bias=div_eps[:, 0:1], scale=1.0)
+                else:
+                    nc.vector.tensor_scalar(out=sg_keep[s][:, tiles, :], in0=nt_keep[s][:, tiles, :],
+                                            scalar1=-DIV_EPS, scalar2=0.5,
+                                            op0=ALU.is_ge, op1=ALU.subtract)
 
             order = (GF, GZ, GI, GO)
             for n, g in enumerate(order):
@@ -444,32 +446,18 @@ def tile_slstmblock_pa_t_kernel(
                         normalise(2, 1, nc.gpsimd)
                     normalise(ahead, first, nc.gpsimd)
                     normalise(ahead, first + 1, nc.gpsimd)
-                if nxt:
-                    fill(i + 1, GF)
                 if more:
-                    gate_product(s + 1, HEADS * pairs[0])
-                if nxt:
-                    fill(i + 1, GZ)
-                if more:
-                    gate_product(s + 1, HEADS * pairs[0] + 1)
+                    for g in pairs:
+                        gate_product(s + 1, HEADS * g)
+                        gate_product(s + 1, HEADS * g + 1)
                 if s + 2 < N_CHUNKS:
                     turn_x(s + 2, PAIR * q)
-                if q == 0 and nxt:
-                    fill(i + 1, GI)
-                if more:
-                    gate_product(s + 1, HEADS * pairs[1])
+                    turn_x(s + 2, PAIR * q + 1)
                 if q == 0 and more:
                     turn_h(s + 1)
-                if q == 1 and nxt:
-                    fill(i + 1, GI)
-                if more:
-                    gate_product(s + 1, HEADS * pairs[1] + 1)
-                if q == 0 and nxt:
-                    fill(i + 1, GO)
-                if s + 2 < N_CHUNKS:
-                    turn_x(s + 2, PAIR * q + 1)
-                if q == 1 and nxt:
-                    fill(i + 1, GO)
+                if nxt:
+                    for g in (GF, GI, GZ, GO):
+                        fill(i + 1, g)
                 if i >= 2:
                     c_last(i - 2)
                 if later < N_CHUNKS:
@@ -527,9 +515,12 @@ def tile_slstmblock_pa_t_kernel(
                 for tiles in halves:
                     nc.scalar.activation(out=nt_keep[s][:, tiles, :], in_=nt_keep[s][:, tiles, :],
                                          func=ACT.Square)
-                for tiles in halves:
-                    nc.vector.tensor_tensor(out=oc_keep[s][:, tiles, :], in0=oc_keep[s][:, tiles, :],
-                                            in1=nt_keep[s][:, tiles, :], op=ALU.mult)
+                for q, tiles in enumerate(halves):
+                    nc.vector.scalar_tensor_tensor(out=oc_keep[s][:, tiles, :],
+                                                   in0=oc_keep[s][:, tiles, :],
+                                                   scalar=0.5 if q == 0 else 1.0,
+                                                   in1=nt_keep[s][:, tiles, :],
+                                                   op0=ALU.mult, op1=ALU.mult)
                 for tiles in halves:
                     nc.vector.tensor_tensor(out=oc_keep[s][:, tiles, :], in0=oc_keep[s][:, tiles, :],
                                             in1=sg_keep[s][:, tiles, :], op=ALU.mult)

@@ -97,7 +97,10 @@ def tile_slstmblock_pa_t_kernel(
             nc.sync.dma_start(out=n_sb[:], in_=chunk_rows(n_prev, s))
             n_tiles[s] = n_sb
 
-        load_x(0)
+        x_first = loads.tile([P, TILES, D_IN], BF16, tag="x_sb", bufs=3, name="x_first")
+        for j in range(TILES):
+            nc.sync.dma_start(out=x_first[:, j, :], in_=chunk_rows(x, 0)[:, j, :])
+        x_tiles[0] = x_first
 
         vec_rows = const.tile([P, P], BF16)
         nc.vector.memset(vec_rows[:], 0.0)
@@ -139,15 +142,15 @@ def tile_slstmblock_pa_t_kernel(
                 stats_of[s] = ln_pool.tile([P, TILES, 6], F32, tag="stats", name="stats")
             nc.vector.bn_stats(out=stats_of[s][:, j, :], in_=x_tiles[s][:, j, :])
 
-        def finish_statistics(s):
+        def finish_statistics(s, engine=nc.gpsimd):
             stats = stats_of.pop(s)
             mean_var = ln_pool.tile([P, TILES, 2], F32, tag="mean_var")
             for j in range(TILES):
                 nc.vector.bn_aggr(out=mean_var[:, j, :], in_=stats[:, j, :])
             var_eps = ln_pool.tile([P, TILES], F32, tag="var_eps")
-            nc.gpsimd.tensor_scalar_add(out=var_eps[:], in0=mean_var[:, :, 1], scalar1=LN_EPS)
+            engine.tensor_scalar_add(out=var_eps[:], in0=mean_var[:, :, 1], scalar1=LN_EPS)
             neg_mean = ln_pool.tile([P, TILES], F32, tag="neg_mean")
-            nc.gpsimd.tensor_scalar_mul(out=neg_mean[:], in0=mean_var[:, :, 0], scalar1=-1.0)
+            engine.tensor_scalar_mul(out=neg_mean[:], in0=mean_var[:, :, 0], scalar1=-1.0)
             rstd = ln_pool.tile([P, TILES], F32, tag="rstd")
             nc.gpsimd.tensor_tensor(out=rstd[:], in0=var_eps[:], in1=neg_half[:], op=ALU.pow)
             scale_of[s] = (neg_mean, rstd)
@@ -231,7 +234,7 @@ def tile_slstmblock_pa_t_kernel(
                 nc.gpsimd.tensor_copy(out=ln_cols[:, PACK:2 * PACK], in_=lnb_rows[:])
                 for j in range(TILES):
                     statistics(0, j)
-                finish_statistics(0)
+                finish_statistics(0, nc.vector)
                 group_weights(GF, nc.scalar.copy)
                 group_weights(GZ, nc.scalar.copy)
                 group_weights(GO, nc.scalar.copy)

@@ -77,7 +77,7 @@ def tile_slstmblock_pa_t_kernel(
         m_tiles = {}
 
         def load_x(s):
-            x_sb = loads.tile([P, TILES, D_IN], BF16, tag="x_sb", bufs=3)
+            x_sb = loads.tile([P, TILES, D_IN], BF16, tag="x_sb", bufs=4)
             nc.sync.dma_start(out=x_sb[:], in_=chunk_rows(x, s))
             x_tiles[s] = x_sb
 
@@ -97,7 +97,7 @@ def tile_slstmblock_pa_t_kernel(
             nc.sync.dma_start(out=n_sb[:], in_=chunk_rows(n_prev, s))
             n_tiles[s] = n_sb
 
-        x_first = loads.tile([P, TILES, D_IN], BF16, tag="x_sb", bufs=3, name="x_first")
+        x_first = loads.tile([P, TILES, D_IN], BF16, tag="x_sb", bufs=4, name="x_first")
         for j in range(TILES):
             nc.sync.dma_start(out=x_first[:, j, :], in_=chunk_rows(x, 0)[:, j, :])
         x_tiles[0] = x_first
@@ -142,7 +142,7 @@ def tile_slstmblock_pa_t_kernel(
                 stats_of[s] = ln_pool.tile([P, TILES, 6], F32, tag="stats", name="stats")
             nc.vector.bn_stats(out=stats_of[s][:, j, :], in_=x_tiles[s][:, j, :])
 
-        def finish_statistics(s, engine=nc.gpsimd):
+        def finish_statistics(s, engine=nc.vector):
             stats = stats_of.pop(s)
             mean_var = ln_pool.tile([P, TILES, 2], F32, tag="mean_var")
             for j in range(TILES):
@@ -210,12 +210,14 @@ def tile_slstmblock_pa_t_kernel(
                 w_raw = setup.tile([P, PACK, D_HID], BF16)
                 nc.sync.dma_start(out=w_raw[:], in_=weights[g].rearrange("(p t) f -> p t f", t=PACK))
                 w_raw_tiles.append(w_raw)
-            load_x(1)
+                if g == 1:
+                    load_x(1)
             load_h(0)
             for g in range(GATES):
                 nc.sync.dma_start(out=r_sb[:, g, :, :], in_=recurrents[g].rearrange("h k f -> k h f"))
             load_x(2)
             load_state(0)
+            load_x(3)
             w_grouped_tiles = {}
 
             def group_weights(g, copy):
@@ -230,8 +232,8 @@ def tile_slstmblock_pa_t_kernel(
                                       in_=w_grouped_tiles[g][:].rearrange("p f t -> p (f t)"))
 
             with ExitStack():
-                nc.gpsimd.tensor_copy(out=ln_cols[:, 0:PACK], in_=lnw_rows[:])
-                nc.gpsimd.tensor_copy(out=ln_cols[:, PACK:2 * PACK], in_=lnb_rows[:])
+                nc.scalar.copy(out=ln_cols[:, 0:PACK], in_=lnw_rows[:])
+                nc.scalar.copy(out=ln_cols[:, PACK:2 * PACK], in_=lnb_rows[:])
                 for j in range(TILES):
                     statistics(0, j)
                 finish_statistics(0, nc.vector)
@@ -242,8 +244,7 @@ def tile_slstmblock_pa_t_kernel(
                 vec_ps = psum_rot.tile([P, P], BF16, tag="turn")
                 nc.tensor.transpose(vec_ps[:], vec_rows[:], ident_bf16[:])
                 nc.scalar.copy(out=vec_cols[:], in_=vec_ps[:, 0:24])
-                nc.gpsimd.tensor_tensor(out=gate_bias[:], in0=vec_cols[:, 8:16],
-                                        in1=vec_cols[:, 16:24], op=ALU.add)
+                nc.vector.tensor_add(out=gate_bias[:], in0=vec_cols[:, 8:16], in1=vec_cols[:, 16:24])
                 quantise_weights(GZ)
                 quantise_weights(GF)
                 for j in range(TILES):
@@ -262,9 +263,8 @@ def tile_slstmblock_pa_t_kernel(
                 quantise(0)
                 finish_statistics(1)
                 for j in range(TILES):
-                    normalise(1, j, nc.gpsimd)
+                    normalise(1, j, nc.vector)
                 turn_h(0)
-                load_x(3)
 
         with ExitStack():
             gate = stack.enter_context(tc.tile_pool(name="gate", bufs=2, reuse_waits="tile"))

from contextlib import ExitStack

import concourse.mybir as mybir
from concourse.masks import make_identity

F32 = mybir.dt.float32
BF16 = mybir.dt.bfloat16
U32 = mybir.dt.uint32
U8 = mybir.dt.uint8
FP8X4 = mybir.dt.float8_e4m3fn_x4
ALU = mybir.AluOpType
ACT = mybir.ActivationFunctionType
PE = mybir.EngineType.PE
SCALAR = mybir.EngineType.Activation
VECTOR = mybir.EngineType.DVE
GPSIMD = mybir.EngineType.Pool

P = 128
PACK = 4
ROWS = 4096
D_IN = 512
D_HID = 256
HEADS = 2
D_HEAD = 128
GATES = 4
BLOCKS = GATES * HEADS
LN_EPS = 1e-5
DIV_EPS = 1e-13

TILES = 4
CHUNK = TILES * P
N_CHUNKS = ROWS // CHUNK
PAIR = 2
N_PAIRS = TILES // PAIR
N_HALVES = N_CHUNKS * N_PAIRS

FLOPS = 2 * ROWS * D_IN * GATES * D_HID + 2 * ROWS * D_HEAD * GATES * D_HID


def tile_slstmblock_pa_t_kernel(
    tc, x, h_prev, c_prev, n_prev, m_prev, ln_w, ln_b,
    Wz, b_z, Rz, rb_z, Wi, b_i, Ri, rb_i, Wf, b_f, Rf, rb_f, Wo, b_o, Ro, rb_o,
    out_0, out_1, out_2, out_3,
):
    nc = tc.nc
    weights = [Wz, Wi, Wf, Wo]
    recurrents = [Rz, Ri, Rf, Ro]
    biases = [b_z, b_i, b_f, b_o]
    rec_biases = [rb_z, rb_i, rb_f, rb_o]
    GZ, GI, GF, GO = 0, 1, 2, 3

    def chunk_rows(dram, s):
        return dram[s * CHUNK:(s + 1) * CHUNK, :].rearrange("(p j) w -> p j w", j=TILES)

    with ExitStack() as stack:
        const = stack.enter_context(tc.tile_pool(name="const", bufs=1))
        keep = stack.enter_context(tc.tile_pool(name="keep", bufs=1))
        loads = stack.enter_context(tc.tile_pool(name="loads", bufs=2))
        psum_pre = stack.enter_context(tc.psum_pool(name="psum_pre", bufs=1))
        psum_rot = stack.enter_context(tc.psum_pool(name="psum_rot", bufs=2))

        div_eps = const.tile([P, 1], F32)
        nc.vector.memset(div_eps[:], DIV_EPS)
        warm = const.tile([P, 1], F32)
        nc.scalar.activation(out=warm[:], in_=div_eps[:], func=ACT.Exp)
        ident_f32 = const.tile([P, P], F32)
        make_identity(nc, ident_f32[:])
        ident_bf16 = const.tile([P, P], BF16)
        make_identity(nc, ident_bf16[:])
        neg_half = const.tile([P, TILES], F32)
        nc.vector.memset(neg_half[:], -0.5)

        x_tiles = {}
        h_tiles = {}
        c_tiles = {}
        n_tiles = {}
        m_tiles = {}

        def load_x(s):
            x_sb = loads.tile([P, TILES, D_IN], BF16, tag="x_sb", bufs=4)
            nc.sync.dma_start(out=x_sb[:], in_=chunk_rows(x, s))
            x_tiles[s] = x_sb

        def load_h(s):
            h_sb = loads.tile([P, TILES, D_HID], BF16, tag="h_sb")
            nc.sync.dma_start(out=h_sb[:], in_=chunk_rows(h_prev, s))
            h_tiles[s] = h_sb

        def load_state(s):
            m_sb = loads.tile([P, TILES, D_HID], BF16, tag="m_sb")
            nc.sync.dma_start(out=m_sb[:], in_=chunk_rows(m_prev, s))
            m_tiles[s] = m_sb
            c_sb = loads.tile([P, TILES, D_HID], BF16, tag="c_sb")
            nc.sync.dma_start(out=c_sb[:], in_=chunk_rows(c_prev, s))
            c_tiles[s] = c_sb
            n_sb = loads.tile([P, TILES, D_HID], BF16, tag="n_sb")
            nc.sync.dma_start(out=n_sb[:], in_=chunk_rows(n_prev, s))
            n_tiles[s] = n_sb

        x_first = loads.tile([P, TILES, D_IN], BF16, tag="x_sb", bufs=4, name="x_first")
        for j in range(TILES):
            nc.sync.dma_start(out=x_first[:, j, :], in_=chunk_rows(x, 0)[:, j, :])
        x_tiles[0] = x_first

        vec_rows = const.tile([P, P], BF16)
        nc.vector.memset(vec_rows[:], 0.0)
        lnw_rows = const.tile([P, PACK], BF16)
        nc.scalar.dma_start(out=lnw_rows[:], in_=ln_w.rearrange("(p t) -> p t", t=PACK))
        lnb_rows = const.tile([P, PACK], BF16)
        nc.scalar.dma_start(out=lnb_rows[:], in_=ln_b.rearrange("(p t) -> p t", t=PACK))
        for g in range(GATES):
            nc.scalar.dma_start(out=vec_rows[8 + HEADS * g:8 + HEADS * (g + 1), :],
                                in_=biases[g].rearrange("(h f) -> h f", f=D_HEAD))
            nc.scalar.dma_start(out=vec_rows[16 + HEADS * g:16 + HEADS * (g + 1), :],
                                in_=rec_biases[g].rearrange("(h f) -> h f", f=D_HEAD))

        w_codes = const.tile([P, GATES * D_HID], U32, align_bytes=64)
        w_scales = const.tile([P, GATES * D_HID], U8, align_bytes=64)
        r_sb = const.tile([P, GATES, HEADS, D_HEAD], BF16)
        ln_cols = const.tile([P, 2 * PACK], F32)
        vec_cols = const.tile([P, 24], F32)
        gate_bias = const.tile([P, BLOCKS], F32)
        gain = ln_cols[:, 0:PACK]
        shift = ln_cols[:, PACK:2 * PACK]

        nt_keep = [keep.tile([P, TILES, D_HID], F32, name="nt_keep%d" % s) for s in range(N_CHUNKS)]
        oc_keep = [keep.tile([P, TILES, D_HID], F32, name="oc_keep%d" % s) for s in range(N_CHUNKS)]
        sg_keep = [keep.tile([P, TILES, D_HID], BF16, name="sg_keep%d" % s) for s in range(N_CHUNKS)]

        ln_pool = stack.enter_context(tc.tile_pool(name="ln_pool", bufs=2, reuse_waits="tile"))
        stats_of = {}
        scale_of = {}
        xh_tiles = {}
        planes_of = {}
        grouped_of = {}
        x_mx = {}
        ht_tiles = {}
        mt_tiles = {}

        def statistics(s, j):
            if j == 0:
                stats_of[s] = ln_pool.tile([P, TILES, 6], F32, tag="stats", name="stats")
            nc.vector.bn_stats(out=stats_of[s][:, j, :], in_=x_tiles[s][:, j, :])

        def finish_statistics(s, engine=nc.vector):
            stats = stats_of.pop(s)
            mean_var = ln_pool.tile([P, TILES, 2], F32, tag="mean_var")
            for j in range(TILES):
                nc.vector.bn_aggr(out=mean_var[:, j, :], in_=stats[:, j, :])
            var_eps = ln_pool.tile([P, TILES], F32, tag="var_eps")
            engine.tensor_scalar_add(out=var_eps[:], in0=mean_var[:, :, 1], scalar1=LN_EPS)
            neg_mean = ln_pool.tile([P, TILES], F32, tag="neg_mean")
            engine.tensor_scalar_mul(out=neg_mean[:], in0=mean_var[:, :, 0], scalar1=-1.0)
            rstd = ln_pool.tile([P, TILES], F32, tag="rstd")
            nc.gpsimd.tensor_tensor(out=rstd[:], in0=var_eps[:], in1=neg_half[:], op=ALU.pow)
            scale_of[s] = (neg_mean, rstd)
            xh_tiles[s] = []

        def normalise(s, j, engine):
            neg_mean, rstd = scale_of[s]
            xh_j = ln_pool.tile([P, D_IN], F32, tag="xh", bufs=2 * TILES)
            engine.tensor_scalar(out=xh_j[:].rearrange("p (t k) -> p t k", t=PACK),
                                 in0=x_tiles[s][:, j, :].rearrange("p (k t) -> p t k", t=PACK),
                                 scalar1=neg_mean[:, j:j + 1], scalar2=rstd[:, j:j + 1],
                                 op0=ALU.add, op1=ALU.mult)
            xh_tiles[s].append(xh_j)

        def turn_x(s, t, on_vector=False):
            if t == 0:
                planes_of[s] = ln_pool.tile([P, PACK, CHUNK], BF16, tag="planes", bufs=1, name="planes")
            turned = psum_rot.tile([P, CHUNK], F32, tag="turn")
            for j in range(TILES):
                nc.tensor.transpose(turned[:, j * P:(j + 1) * P],
                                    xh_tiles[s][j][:, t * P:(t + 1) * P], ident_f32[:])
            if on_vector:
                nc.vector.tensor_scalar(out=planes_of[s][:, t, :], in0=turned[:],
                                        scalar1=gain[:, t:t + 1], scalar2=shift[:, t:t + 1],
                                        op0=ALU.mult, op1=ALU.add)
            else:
                nc.scalar.activation(out=planes_of[s][:, t, :], in_=turned[:], func=ACT.Identity,
                                     bias=shift[:, t:t + 1], scale=gain[:, t:t + 1])

        def regroup(s):
            grouped = ln_pool.tile([P, CHUNK, PACK], BF16, tag="grouped", bufs=1, align_bytes=64)
            nc.vector.tensor_copy(out=grouped[:].rearrange("p (c i) t -> p c t i", i=4),
                                  in_=planes_of.pop(s)[:].rearrange("p t (c i) -> p c t i", i=4))
            grouped_of[s] = grouped

        def quantise(s):
            x_codes = ln_pool.tile([P, CHUNK], U32, tag="x_codes", align_bytes=64)
            x_scales = ln_pool.tile([P, CHUNK], U8, tag="x_scales", align_bytes=64)
            nc.vector.quantize_mx(out=x_codes[:].bitcast(FP8X4), scales=x_scales[:],
                                  in_=grouped_of.pop(s)[:].rearrange("p r t -> p (r t)"))
            x_mx[s] = (x_codes, x_scales)

        def turn_h(s):
            h_sb = h_tiles.pop(s)
            h_ps = psum_rot.tile([P, HEADS, TILES, P], BF16, tag="turn")
            for h in range(HEADS):
                for j in range(TILES):
                    nc.tensor.transpose(h_ps[:, h, j, :],
                                        h_sb[:, j, h * D_HEAD:(h + 1) * D_HEAD], ident_bf16[:])
            h_turned = ln_pool.tile([P, HEADS, TILES, P], BF16, tag="h_turned")
            nc.scalar.copy(out=h_turned[:], in_=h_ps[:])
            ht_tiles[s] = h_turned

        with tc.tile_pool(name="setup", bufs=GATES) as setup:
            w_raw_tiles = []
            for g in range(GATES):
                w_raw = setup.tile([P, PACK, D_HID], BF16)
                nc.sync.dma_start(out=w_raw[:], in_=weights[g].rearrange("(p t) f -> p t f", t=PACK))
                w_raw_tiles.append(w_raw)
                if g == 1:
                    load_x(1)
            load_h(0)
            for g in range(GATES):
                nc.sync.dma_start(out=r_sb[:, g, :, :], in_=recurrents[g].rearrange("h k f -> k h f"))
            load_x(2)
            load_state(0)
            load_x(3)
            w_grouped_tiles = {}

            def group_weights(g, copy):
                w_grouped = setup.tile([P, D_HID, PACK], BF16, align_bytes=64)
                copy(out=w_grouped[:].rearrange("p (c i) t -> p c t i", i=4),
                     in_=w_raw_tiles[g][:].rearrange("p t (c i) -> p c t i", i=4))
                w_grouped_tiles[g] = w_grouped

            def quantise_weights(g):
                cols = slice(g * D_HID, (g + 1) * D_HID)
                nc.vector.quantize_mx(out=w_codes[:, cols].bitcast(FP8X4), scales=w_scales[:, cols],
                                      in_=w_grouped_tiles[g][:].rearrange("p f t -> p (f t)"))

            with ExitStack():
                nc.scalar.copy(out=ln_cols[:, 0:PACK], in_=lnw_rows[:])
                nc.scalar.copy(out=ln_cols[:, PACK:2 * PACK], in_=lnb_rows[:])
                for j in range(TILES):
                    statistics(0, j)
                finish_statistics(0, nc.vector)
                group_weights(GF, nc.scalar.copy)
                group_weights(GZ, nc.scalar.copy)
                group_weights(GO, nc.scalar.copy)
                group_weights(GI, nc.scalar.copy)
                vec_ps = psum_rot.tile([P, P], BF16, tag="turn")
                nc.tensor.transpose(vec_ps[:], vec_rows[:], ident_bf16[:])
                nc.scalar.copy(out=vec_cols[:], in_=vec_ps[:, 0:24])
                nc.vector.tensor_add(out=gate_bias[:], in0=vec_cols[:, 8:16], in1=vec_cols[:, 16:24])
                quantise_weights(GZ)
                quantise_weights(GF)
                for j in range(TILES):
                    normalise(0, j, nc.vector)
                turn_x(0, 0)
                quantise_weights(GI)
                quantise_weights(GO)
                statistics(1, 0)
                turn_x(0, 1)
                turn_x(0, 2)
                statistics(1, 1)
                turn_x(0, 3)
                statistics(1, 2)
                regroup(0)
                statistics(1, 3)
                quantise(0)
                finish_statistics(1)
                for j in range(TILES):
                    normalise(1, j, nc.vector)
                turn_h(0)

        with ExitStack():
            gate = stack.enter_context(tc.tile_pool(name="gate", bufs=2, reuse_waits="tile"))

            def gate_product(s, blk, on_vector=False):
                x_codes, x_scales = x_mx[s]
                if s not in mt_tiles:
                    mt_tiles[s] = gate.tile([P, BLOCKS, CHUNK], F32, tag="mx_turned",
                                            name="mx_turned")
                cols = slice(blk * P, (blk + 1) * P)
                mx_ps = psum_rot.tile([P, CHUNK], F32, tag="mx_ps")
                nc.tensor.matmul_mx(out=mx_ps[:],
                                    lhsT=w_codes[:, cols].bitcast(FP8X4),
                                    lhsT_scale=w_scales[:, cols],
                                    rhs=x_codes[:].bitcast(FP8X4), rhs_scale=x_scales[:],
                                    start=True, stop=True)
                if on_vector:
                    nc.vector.tensor_scalar_add(out=mt_tiles[s][:, blk, :], in0=mx_ps[:],
                                                scalar1=gate_bias[:, blk:blk + 1])
                else:
                    nc.scalar.activation(out=mt_tiles[s][:, blk, :], in_=mx_ps[:], func=ACT.Identity,
                                         bias=gate_bias[:, blk:blk + 1], scale=1.0)

            shape = [P, PAIR, D_HID]
            pre_of = {}
            fm_of = {}
            d_of = {}
            zt_of = {}
            th_of = {}
            ei_of = {}
            ef_of = {}
            iz_of = {}
            m_out = {}
            c_out = {}

            def tiles_of(i):
                q = i % N_PAIRS
                return i // N_PAIRS, slice(q * PAIR, (q + 1) * PAIR)

            def fill(i, g):
                s, q = i // N_PAIRS, i % N_PAIRS
                quarters = [(jj, h) for jj in range(PAIR) for h in range(HEADS)]
                pre_g = psum_pre.tile(shape, F32, tag="pre%d" % g, name="pre_g")
                for n, (jj, h) in enumerate(quarters):
                    j = q * PAIR + jj
                    nc.tensor.matmul(out=pre_g[:, jj, h * D_HEAD:(h + 1) * D_HEAD],
                                     lhsT=mt_tiles[s][:, g * HEADS + h, j * P:(j + 1) * P],
                                     rhs=ident_f32[:], start=(n == 0), stop=False,
                                     is_transpose=True)
                for n, (jj, h) in enumerate(quarters):
                    j = q * PAIR + jj
                    nc.tensor.matmul(out=pre_g[:, jj, h * D_HEAD:(h + 1) * D_HEAD],
                                     lhsT=ht_tiles[s][:, h, j, :], rhs=r_sb[:, g, h, :],
                                     start=False, stop=(n == len(quarters) - 1))
                pre_of[i, g] = pre_g

            def tanhs(i):
                zt = gate.tile(shape, F32, tag="zt", bufs=3)
                nc.scalar.activation(out=zt[:], in_=pre_of[i, GZ][:], func=ACT.Tanh)
                th = gate.tile(shape, F32, tag="th", bufs=4)
                nc.scalar.activation(out=th[:], in_=pre_of[i, GO][:], func=ACT.Tanh, scale=0.5)
                zt_of[i] = zt
                th_of[i] = th

            def copy_fm(i):
                s, tiles = tiles_of(i)
                fm = gate.tile(shape, F32, tag="fm")
                nc.vector.tensor_tensor(out=fm[:], in0=pre_of[i, GF][:], in1=m_tiles[s][:, tiles, :],
                                        op=ALU.add)
                fm_of[i] = fm

            def difference(i):
                d = gate.tile(shape, F32, tag="d")
                nc.vector.tensor_tensor(out=d[:], in0=pre_of[i, GI][:], in1=fm_of[i][:],
                                        op=ALU.subtract)
                d_of[i] = d

            def maximum(i):
                s, tiles = tiles_of(i)
                if i % N_PAIRS == 0:
                    m_out[s] = gate.tile([P, TILES, D_HID], F32, tag="m_stage", name="m_stage")
                nc.vector.tensor_tensor(out=m_out[s][:, tiles, :], in0=pre_of[i, GI][:],
                                        in1=fm_of.pop(i)[:], op=ALU.max)

            def exps(i):
                e_f = gate.tile(shape, F32, tag="e_f")
                nc.scalar.activation(out=e_f[:], in_=d_of[i][:], func=ACT.Exp, scale=-1.0)
                e_i = gate.tile(shape, F32, tag="e_i")
                nc.scalar.activation(out=e_i[:], in_=d_of.pop(i)[:], func=ACT.Exp)
                ei_of[i] = e_i
                ef_of[i] = e_f

            def c_first(i):
                s, tiles = tiles_of(i)
                if i % N_PAIRS == 0:
                    c_out[s] = gate.tile([P, TILES, D_HID], F32, tag="c_stage", name="c_stage")
                nc.vector.scalar_tensor_tensor(out=c_out[s][:, tiles, :], in0=ef_of[i][:], scalar=1.0,
                                               in1=c_tiles[s][:, tiles, :],
                                               op0=ALU.min, op1=ALU.mult)

            def n_first(i):
                s, tiles = tiles_of(i)
                nc.vector.scalar_tensor_tensor(out=nt_keep[s][:, tiles, :], in0=ef_of.pop(i)[:],
                                               scalar=1.0, in1=n_tiles[s][:, tiles, :],
                                               op0=ALU.min, op1=ALU.mult)

            def n_last(i):
                s, tiles = tiles_of(i)
                nt = nt_keep[s][:, tiles, :]
                nc.vector.scalar_tensor_tensor(out=nt, in0=ei_of[i][:], scalar=1.0, in1=nt,
                                               op0=ALU.min, op1=ALU.add)

            def i_times_z(i):
                iz = gate.tile(shape, F32, tag="iz")
                nc.vector.scalar_tensor_tensor(out=iz[:], in0=ei_of.pop(i)[:], scalar=1.0,
                                               in1=zt_of.pop(i)[:], op0=ALU.min, op1=ALU.mult)
                iz_of[i] = iz

            def c_last(i):
                s, tiles = tiles_of(i)
                ct = c_out[s][:, tiles, :]
                nc.vector.tensor_tensor(out=ct, in0=ct, in1=iz_of.pop(i)[:], op=ALU.add)

            def o_times_c(i):
                s, tiles = tiles_of(i)
                nc.vector.scalar_tensor_tensor(out=oc_keep[s][:, tiles, :], in0=th_of.pop(i)[:],
                                               scalar=1.0, in1=c_out[s][:, tiles, :],
                                               op0=ALU.add, op1=ALU.mult)

            def half_sign(i):
                s, tiles = tiles_of(i)
                if i % N_PAIRS == 0:
                    nc.scalar.activation(out=sg_keep[s][:, tiles, :], in_=nt_keep[s][:, tiles, :],
                                         func=ACT.Sign, bias=div_eps[:, 0:1], scale=1.0)
                else:
                    nc.vector.tensor_scalar(out=sg_keep[s][:, tiles, :], in0=nt_keep[s][:, tiles, :],
                                            scalar1=-DIV_EPS, scalar2=0.5,
                                            op0=ALU.is_ge, op1=ALU.subtract)

            order = (GF, GZ, GI, GO)
            for n, g in enumerate(order):
                gate_product(0, HEADS * g)
                gate_product(0, HEADS * g + 1)
                if n >= 1:
                    fill(0, order[n - 1])
            fill(0, order[-1])
            for j in range(TILES):
                statistics(2, j)
            finish_statistics(2)
            load_x(4)
            statistics(3, 0)
            statistics(3, 1)

            def half(i):
                s, q = i // N_PAIRS, i % N_PAIRS
                if q == 0:
                    if s + 1 < N_CHUNKS:
                        load_h(s + 1)
                        load_state(s + 1)
                elif s + 5 < N_CHUNKS:
                    load_x(s + 5)
                more = s + 1 < N_CHUNKS
                nxt = i + 1 < N_HALVES
                pairs = (GF, GZ) if q == 0 else (GI, GO)
                ahead = s + 2 + q
                later = s + 3 + q
                first = PAIR * (1 - q)
                if i == 0:
                    for t in range(PACK):
                        turn_x(1, t)
                    regroup(1)
                copy_fm(i)
                tanhs(i)
                if q == 0 and more:
                    quantise(s + 1)
                difference(i)
                exps(i)
                maximum(i)
                if ahead < N_CHUNKS:
                    if i == 0:
                        normalise(2, 0, nc.gpsimd)
                        normalise(2, 1, nc.gpsimd)
                    normalise(ahead, first, nc.gpsimd)
                    normalise(ahead, first + 1, nc.gpsimd)
                if more:
                    for g in pairs:
                        gate_product(s + 1, HEADS * g)
                        gate_product(s + 1, HEADS * g + 1)
                if s + 2 < N_CHUNKS:
                    turn_x(s + 2, PAIR * q)
                    turn_x(s + 2, PAIR * q + 1)
                if q == 0 and more:
                    turn_h(s + 1)
                if nxt:
                    for g in (GF, GI, GZ, GO):
                        fill(i + 1, g)
                if i >= 2:
                    c_last(i - 2)
                if later < N_CHUNKS:
                    statistics(later, first)
                    statistics(later, first + 1)
                if i >= 1:
                    c_first(i - 1)
                    n_first(i - 1)
                if i >= 2:
                    o_times_c(i - 2)
                if i >= 1:
                    n_last(i - 1)
                if i >= 2:
                    half_sign(i - 2)
                if i >= 1:
                    i_times_z(i - 1)
                if q == 0:
                    if later < N_CHUNKS:
                        finish_statistics(later)
                    if s >= 1:
                        nc.sync.dma_start(out=chunk_rows(out_2, s - 1), in_=nt_keep[s - 1][:])
                else:
                    if s + 2 < N_CHUNKS:
                        regroup(s + 2)
                    nc.sync.dma_start(out=chunk_rows(out_3, s), in_=m_out.pop(s)[:])
                    if s >= 1:
                        nc.sync.dma_start(out=chunk_rows(out_1, s - 1), in_=c_out.pop(s - 1)[:])

            for i in range(N_HALVES - 2):
                half(i)
            stack.enter_context(tc.manual_schedule(engines={SCALAR}))
            half(N_HALVES - 2)
            half(N_HALVES - 1)

            halves = [slice(q * PAIR, (q + 1) * PAIR) for q in range(N_PAIRS)]
            last = N_CHUNKS - 1
            final = N_HALVES - 1
            c_last(final - 1)
            c_first(final)
            n_first(final)
            o_times_c(final - 1)
            n_last(final)
            half_sign(final - 1)
            i_times_z(final)
            nc.sync.dma_start(out=chunk_rows(out_2, last), in_=nt_keep[last][:])
            c_last(final)
            nc.sync.dma_start(out=chunk_rows(out_1, last), in_=c_out[last][:])
            for s in range(N_CHUNKS):
                if s == 1:
                    half_sign(final)
                    o_times_c(final)
                for tiles in halves:
                    nc.scalar.activation(out=nt_keep[s][:, tiles, :], in_=nt_keep[s][:, tiles, :],
                                         func=ACT.Abs_reciprocal_sqrt, bias=div_eps[:, 0:1], scale=1.0)
                for tiles in halves:
                    nc.scalar.activation(out=nt_keep[s][:, tiles, :], in_=nt_keep[s][:, tiles, :],
                                         func=ACT.Square)
                for q, tiles in enumerate(halves):
                    nc.vector.scalar_tensor_tensor(out=oc_keep[s][:, tiles, :],
                                                   in0=oc_keep[s][:, tiles, :],
                                                   scalar=0.5 if q == 0 else 1.0,
                                                   in1=nt_keep[s][:, tiles, :],
                                                   op0=ALU.mult, op1=ALU.mult)
                for tiles in halves:
                    nc.vector.tensor_tensor(out=oc_keep[s][:, tiles, :], in0=oc_keep[s][:, tiles, :],
                                            in1=sg_keep[s][:, tiles, :], op=ALU.mult)
                    if s == last:
                        nc.sync.dma_start(out=chunk_rows(out_0, s)[:, tiles, :],
                                          in_=oc_keep[s][:, tiles, :])
                if s < last:
                    nc.sync.dma_start(out=chunk_rows(out_0, s), in_=oc_keep[s][:])
